import numpy as np
import ml_dtypes


def mxq(x, axis, fmt="e4m3"):
    dtype, down = {"e4m3": (ml_dtypes.float8_e4m3fn, 7), "e5m2": (ml_dtypes.float8_e5m2, 14)}[fmt]
    v = np.moveaxis(np.asarray(x, np.float32).astype(ml_dtypes.bfloat16).astype(np.float64), axis, -1)
    blocks = v.reshape(v.shape[:-1] + (-1, 32))
    amax = np.abs(blocks).max(-1, keepdims=True)
    byte = np.maximum(np.where(amax > 0, np.frexp(amax)[1] - 1 + 127, 0) - down, 1)
    scale = np.exp2(byte - 127.0)
    codes = (blocks / scale).astype(np.float32).astype(dtype).astype(np.float64)
    return np.moveaxis((codes * scale).reshape(v.shape), -1, axis)


WIDE = False


def mx_kscale(k):
    if not WIDE:
        return np.ones(k)
    levels = np.array([10, -10, 5, -5, 0])
    a = np.random.permutation(np.resize(levels, k // 512 * 4)).reshape(k // 512, 4)
    idx = np.arange(k)
    return np.exp2(a[idx // 512, idx % 128 // 32])


BF16 = ml_dtypes.bfloat16


def bf(x):
    return np.asarray(x, np.float32).astype(BF16)


def f64(x):
    return np.asarray(x).astype(np.float64)


N, M, D, B = 256, 512, 4, 1024
MD = M * D


def sigmoid(v):
    return 1.0 / (1.0 + np.exp(-v))


def diag_mask():
    return np.broadcast_to((1.0 - np.eye(M))[:, :, None], (M, M, D)).reshape(M, MD)


def tri_mask():
    return f64(np.arange(D)[:, None] < np.arange(D)[None, :])


def big_diag(w):
    w3 = w.reshape(M, M, D).copy()
    i = np.arange(M)
    w3[i, i, :] = np.random.standard_normal((M, D)) * 0.5
    return w3.reshape(M, MD)


def setup_inputs():
    r = np.random.standard_normal
    s = mx_kscale(M)
    ca, cb = 0.7 / np.sqrt(M), 0.7 / np.sqrt(N)
    return {"x_t": bf(r((B, N))), "m_t": bf(r((B, M)) * s), "a_t": bf(r((B, MD))),
            "A_fg": bf(r((M, MD)) * ca / s[:, None]), "A_in": bf(r((M, MD)) * ca / s[:, None]),
            "A_th": bf(big_diag(r((M, MD)) * ca)), "A_pt_blk": bf(r((M, D, D)) * 0.4),
            "B_fg": bf(r((N, MD)) * cb), "B_in": bf(r((N, MD)) * cb), "B_th": bf(r((N, MD)) * cb),
            "b_fg": bf(r((1, MD)) * 0.3), "b_in": bf(r((1, MD)) * 0.3), "b_th": bf(r((1, MD)) * 0.3)}


def reference(x_t, m_t, a_t, A_fg, A_in, A_th, A_pt_blk, B_fg, B_in, B_th, b_fg, b_in, b_th):
    x, a = f64(x_t), f64(a_t)
    mq = mxq(f64(m_t), 1, "e4m3")
    G_fg = sigmoid((mq @ mxq(f64(A_fg), 0, "e4m3")) + x @ f64(B_fg) + f64(b_fg))
    G_in = sigmoid((mq @ mxq(f64(A_in), 0, "e4m3")) + x @ f64(B_in) + f64(b_in))
    a3 = a.reshape(B, M, D)
    P = f64(A_pt_blk) * tri_mask()
    pt = np.zeros((B, M, D))
    for s in range(D):
        pt = pt + a3[:, :, s, None] * P[None, :, s, :]
    a_last = a3[:, :, -1]
    G_th = np.tanh(pt.reshape(B, MD) + (mxq(a_last, 1, "e4m3") @ mxq(f64(A_th) * diag_mask(), 0, "e4m3"))
                   + x @ f64(B_th) + f64(b_th))
    return a * G_fg + G_th * G_in

@@ -1,0 +1,289 @@
+from contextlib import ExitStack
+
+import concourse.mybir as mybir
+from concourse.masks import make_identity
+
+F32 = mybir.dt.float32
+BF16 = mybir.dt.bfloat16
+U32 = mybir.dt.uint32
+U8 = mybir.dt.uint8
+FP8X4 = mybir.dt.float8_e4m3fn_x4
+ADD = mybir.AluOpType.add
+MULT = mybir.AluOpType.mult
+SIGMOID = mybir.ActivationFunctionType.Sigmoid
+TANH = mybir.ActivationFunctionType.Tanh
+AXIS_X = mybir.AxisListType.X
+
+P = 128
+ROWS = 1024
+Q = ROWS // P
+UNITS = 512
+SLOTS = 4
+MD = UNITS * SLOTS
+NX = 256
+CH = 512
+NCH = MD // CH
+PAIRS = Q // 2
+
+FLOPS = 2 * ROWS * MD * 3 * (UNITS + NX) + 2 * ROWS * UNITS * 6
+
+
+def tile_edrncell_pa_kernel(
+    tc, x_t, m_t, a_t, A_fg, A_in, A_th, A_pt_blk, B_fg, B_in, B_th, b_fg, b_in, b_th, out
+):
+    nc = tc.nc
+    with ExitStack() as ctx:
+        const = ctx.enter_context(tc.tile_pool(name="const", bufs=1))
+        raw = ctx.enter_context(tc.tile_pool(name="raw", bufs=6))
+        grp = ctx.enter_context(tc.tile_pool(name="grp", bufs=3))
+        atp = ctx.enter_context(tc.tile_pool(name="atp", bufs=3))
+        zpool = ctx.enter_context(tc.tile_pool(name="zpool", bufs=4))
+        psum_y = ctx.enter_context(tc.psum_pool(name="psum_y", bufs=3))
+        psum_x = ctx.enter_context(tc.psum_pool(name="psum_x", bufs=3))
+        psum_t = ctx.enter_context(tc.psum_pool(name="psum_t", bufs=2))
+
+        x_v = x_t.rearrange("(p q) k -> p q k", q=Q)
+        m_v = m_t.rearrange("(p q) k -> p q k", q=Q)
+        a_v = a_t.rearrange("(p q) c -> p q c", q=Q)
+        out_v = out.rearrange("(p q) c -> p q c", q=Q)
+        A_v = [w.rearrange("(t p) c -> p t c", p=P) for w in (A_fg, A_in, A_th)]
+        B_v = [w.rearrange("(k p) c -> p k c", p=P) for w in (B_fg, B_in, B_th)]
+
+        ident = const.tile([P, P], BF16)
+        x_raw = const.tile([P, Q, NX], BF16)
+        m_raw = [const.tile([P, 2, UNITS], BF16, name="m_raw%d" % j) for j in range(PAIRS)]
+        a_sb = [const.tile([P, 2, MD], BF16, name="a_sb%d" % j) for j in range(PAIRS)]
+        xT = [const.tile([P, 4, 2, P], BF16, name="xT%d" % h) for h in range(2)]
+        m_codes = [const.tile([P, 2 * P], U32, name="m_codes%d" % j, align_bytes=64) for j in range(PAIRS)]
+        m_scales = [const.tile([P, 2 * P], U8, name="m_scales%d" % j, align_bytes=64) for j in range(PAIRS)]
+        l_codes = [const.tile([P, 2 * P], U32, name="l_codes%d" % j, align_bytes=64) for j in range(PAIRS)]
+        l_scales = [const.tile([P, 2 * P], U8, name="l_scales%d" % j, align_bytes=64) for j in range(PAIRS)]
+        B_sb = [[const.tile([P, 2, CH], BF16, name="B_sb%d_%d" % (g, n)) for n in range(NCH)] for g in range(3)]
+        A_codes = [
+            [const.tile([P, CH], U32, name="A_codes%d_%d" % (g, n), align_bytes=64) for n in range(NCH)]
+            for g in range(3)
+        ]
+        A_scales = [
+            [const.tile([P, CH], U8, name="A_scales%d_%d" % (g, n), align_bytes=64) for n in range(NCH)]
+            for g in range(3)
+        ]
+        bb = [const.tile([P, MD], BF16, name="bb%d" % g) for g in range(2)]
+        pt_raw = const.tile([P, 16, SLOTS], BF16)
+        pt_msk = const.tile([P, 16, SLOTS], F32)
+        p_blk = const.tile([P, 16, P], BF16)
+        b_row = const.tile([P, 16, P], BF16)
+        onehot = const.tile([P, SLOTS], F32)
+        tri = const.tile([P, SLOTS], F32)
+        same_unit = const.tile([P, P // SLOTS], F32)
+        off_diag = const.tile([P, CH], BF16)
+
+        A_raw = {}
+
+        def load_B(g, n):
+            nc.sync.dma_start(out=B_sb[g][n][:], in_=B_v[g][:, :, n * CH : (n + 1) * CH])
+
+        def load_A(g, n):
+            a_raw = raw.tile([P, 4, CH], BF16, tag="a_raw")
+            nc.sync.dma_start(out=a_raw[:], in_=A_v[g][:, :, n * CH : (n + 1) * CH])
+            A_raw[(g, n)] = a_raw
+
+        def load_m(j):
+            nc.sync.dma_start(out=m_raw[j][:], in_=m_v[:, 2 * j : 2 * j + 2, :])
+
+        def load_a(j):
+            nc.sync.dma_start(out=a_sb[j][:], in_=a_v[:, 2 * j : 2 * j + 2, :])
+
+        make_identity(nc, ident[:])
+        nc.vector.memset(b_row[:], 0.0)
+        nc.scalar.dma_start(out=b_row[3:4, :, :], in_=b_th.rearrange("o (c i) -> o c i", i=P))
+        nc.scalar.dma_start(out=pt_raw[:], in_=A_pt_blk.rearrange("(c j) s t -> (j s) c t", j=P // SLOTS))
+        nc.scalar.dma_start(out=bb[0][:], in_=b_fg.rearrange("o n -> (o n)").partition_broadcast(P))
+        nc.scalar.dma_start(out=bb[1][:], in_=b_in.rearrange("o n -> (o n)").partition_broadcast(P))
+        nc.sync.dma_start(out=x_raw[:], in_=x_v)
+        for g in range(3):
+            load_B(g, 0)
+        load_m(0)
+        load_A(0, 0)
+        load_A(1, 0)
+        load_a(0)
+        load_A(2, 0)
+        load_m(1)
+        load_a(1)
+        for g in range(3):
+            load_B(g, 1)
+        for g in range(3):
+            load_A(g, 1)
+        load_m(2)
+        load_a(2)
+        load_m(3)
+        load_a(3)
+
+        nc.vector.tensor_reduce(
+            out=onehot[:], in_=ident[:].rearrange("p (j s) -> p s j", s=SLOTS), axis=AXIS_X, op=ADD
+        )
+        nc.vector.tensor_reduce(
+            out=same_unit[:], in_=ident[:].rearrange("p (j s) -> p j s", s=SLOTS), axis=AXIS_X, op=ADD
+        )
+        nc.vector.memset(tri[:], 0.0)
+        nc.vector.tensor_copy(out=tri[:, 1:2], in_=onehot[:, 0:1])
+        nc.vector.tensor_tensor(out=tri[:, 2:3], in0=tri[:, 1:2], in1=onehot[:, 1:2], op=ADD)
+        nc.vector.tensor_tensor(out=tri[:, 3:4], in0=tri[:, 2:3], in1=onehot[:, 2:3], op=ADD)
+        keep = tri[:, 3:4]
+        one3 = onehot[:, 3:4]
+        nc.vector.tensor_scalar(
+            out=off_diag[:].rearrange("p (i s) -> p i s", s=SLOTS),
+            in0=ident[:].unsqueeze(2).to_broadcast([P, P, SLOTS]),
+            scalar1=-1.0,
+            scalar2=1.0,
+            op0=MULT,
+            op1=ADD,
+        )
+        nc.vector.tensor_tensor(
+            out=pt_msk[:], in0=pt_raw[:], in1=tri[:].unsqueeze(1).to_broadcast([P, 16, SLOTS]), op=MULT
+        )
+        for t in range(SLOTS):
+            nc.vector.tensor_tensor(
+                out=p_blk[:].rearrange("p c (j t) -> p c j t", t=SLOTS)[:, :, :, t],
+                in0=pt_msk[:, :, t : t + 1].to_broadcast([P, 16, P // SLOTS]),
+                in1=same_unit[:].unsqueeze(1).to_broadcast([P, 16, P // SLOTS]),
+                op=MULT,
+            )
+        nc.vector.tensor_tensor(out=p_blk[:], in0=p_blk[:], in1=b_row[:], op=ADD)
+
+        for h in range(2):
+            tp = psum_t.tile([P, 4, 2, P], BF16, tag="tp")
+            for qh in range(4):
+                for k in range(2):
+                    nc.tensor.transpose(tp[:, qh, k, :], x_raw[:, 4 * h + qh, k * P : (k + 1) * P], ident[:])
+            nc.scalar.copy(out=xT[h][:], in_=tp[:])
+
+        def quantise_rows(j, source, codes, scales):
+            tp = psum_t.tile([P, 2, 4, P], BF16, tag="tp")
+            for qq in range(2):
+                for t in range(4):
+                    nc.tensor.transpose(tp[:, qq, t, :], source(qq, t), ident[:])
+            g4 = grp.tile([P, 2, P, 4], BF16, tag="g4", align_bytes=64)
+            nc.scalar.copy(out=g4[:], in_=tp[:].rearrange("p q t b -> p q b t"))
+            nc.vector.quantize_mx(
+                out=codes[j][:].bitcast(FP8X4),
+                scales=scales[j][:],
+                in_=g4[:].rearrange("p q b t -> p (q b t)"),
+            )
+
+        def prep_m(j):
+            quantise_rows(j, lambda qq, t: m_raw[j][:, qq, t * P : (t + 1) * P], m_codes, m_scales)
+
+        def prep_last(j):
+            quantise_rows(
+                j,
+                lambda qq, t: a_sb[j][:, qq, :].rearrange("p (t i s) -> p t i s", t=4, s=SLOTS)[:, t, :, 3],
+                l_codes,
+                l_scales,
+            )
+
+        def prep_weights(g, n, on_vector):
+            a_raw = A_raw[(g, n)]
+            if g == 2:
+                nc.vector.tensor_tensor(out=a_raw[:, n, :], in0=a_raw[:, n, :], in1=off_diag[:], op=MULT)
+            a_grp = grp.tile([P, CH, 4], BF16, tag="a_grp", align_bytes=64)
+            dst = a_grp[:].rearrange("p (c i) t -> p c t i", i=4)
+            src = a_raw[:].rearrange("p t (c i) -> p c t i", i=4)
+            if on_vector:
+                nc.vector.tensor_copy(out=dst, in_=src)
+            else:
+                nc.scalar.copy(out=dst, in_=src)
+            nc.vector.quantize_mx(
+                out=A_codes[g][n][:].bitcast(FP8X4),
+                scales=A_scales[g][n][:],
+                in_=a_grp[:].rearrange("p w t -> p (w t)"),
+            )
+
+        def transpose_a(j, n):
+            tp = psum_t.tile([P, 2, 4, P], BF16, tag="tp")
+            for qq in range(2):
+                for cb in range(4):
+                    c = 4 * n + cb
+                    nc.tensor.transpose(tp[:, qq, cb, :], a_sb[j][:, qq, c * P : (c + 1) * P], ident[:])
+            aT = atp.tile([P, 2, 4, P], BF16, tag="aT")
+            nc.vector.tensor_scalar(out=aT[:], in0=tp[:], scalar1=keep, scalar2=one3, op0=MULT, op1=ADD)
+            return aT
+
+        def plain_stage(j, n, aT, zfi, zt):
+            for qq in range(2):
+                q = 2 * j + qq
+                lhs = [xT[q // 4][:, q % 4, k, :] for k in range(2)]
+                for g in range(2):
+                    y = psum_y.tile([P, CH], F32, tag="y")
+                    nc.tensor.matmul(y[:], lhsT=lhs[0], rhs=B_sb[g][n][:, 0, :], start=True, stop=False)
+                    nc.tensor.matmul(y[:], lhsT=lhs[1], rhs=B_sb[g][n][:, 1, :], start=False, stop=True)
+                    nc.vector.tensor_tensor(
+                        out=zfi[:, g, qq, :], in0=y[:], in1=bb[g][:, n * CH : (n + 1) * CH], op=ADD
+                    )
+                y = psum_y.tile([P, CH], F32, tag="y")
+                nc.tensor.matmul(y[:], lhsT=lhs[0], rhs=B_sb[2][n][:, 0, :], start=True, stop=False)
+                for cb in range(4):
+                    nc.tensor.matmul(
+                        y[:, cb * P : (cb + 1) * P],
+                        lhsT=aT[:, qq, cb, :],
+                        rhs=p_blk[:, 4 * n + cb, :],
+                        start=False,
+                        stop=False,
+                    )
+                nc.tensor.matmul(y[:], lhsT=lhs[1], rhs=B_sb[2][n][:, 1, :], start=False, stop=True)
+                nc.scalar.copy(out=zt[:, qq, :], in_=y[:])
+
+        def mx_stage(j, n, zfi, zt):
+            for qq in range(2):
+                rows = slice(qq * P, (qq + 1) * P)
+                for g in range(3):
+                    codes, scales = (m_codes, m_scales) if g < 2 else (l_codes, l_scales)
+                    acc = psum_x.tile([P, CH], F32, tag="acc")
+                    nc.tensor.matmul_mx(
+                        out=acc[:],
+                        lhsT=codes[j][:, rows].bitcast(FP8X4),
+                        lhsT_scale=scales[j][:, rows],
+                        rhs=A_codes[g][n][:].bitcast(FP8X4),
+                        rhs_scale=A_scales[g][n][:],
+                        start=True,
+                        stop=True,
+                    )
+                    z = zfi[:, g, qq, :] if g < 2 else zt[:, qq, :]
+                    nc.vector.tensor_tensor(out=z, in0=acc[:], in1=z, op=ADD)
+
+        def finish(j, n, zfi, zt):
+            nc.scalar.activation(out=zfi[:], in_=zfi[:], func=SIGMOID)
+            nc.scalar.activation(out=zt[:], in_=zt[:], func=TANH)
+            cols = slice(n * CH, (n + 1) * CH)
+            u = n * PAIRS + j
+            eng = nc.vector if (u % 5 == 0 and u > 0) else nc.gpsimd
+            eng.tensor_tensor(out=zfi[:, 0, :, :], in0=zfi[:, 0, :, :], in1=a_sb[j][:, :, cols], op=MULT)
+            eng.tensor_tensor(out=zt[:], in0=zt[:], in1=zfi[:, 1, :, :], op=MULT)
+            eng.tensor_tensor(out=zfi[:, 0, :, :], in0=zfi[:, 0, :, :], in1=zt[:], op=ADD)
+            nc.sync.dma_start(out=out_v[:, 2 * j : 2 * j + 2, cols], in_=zfi[:, 0, :, :])
+
+        prep_m(0)
+        prep_weights(0, 0, True)
+        prep_weights(1, 0, True)
+        prep_last(0)
+        prep_weights(2, 0, True)
+        for g in range(3):
+            load_B(g, 2)
+        for g in range(3):
+            load_A(g, 2)
+
+        for n in range(NCH):
+            for j in range(PAIRS):
+                aT = transpose_a(j, n)
+                zfi = zpool.tile([P, 2, 2, CH], F32, tag="zfi")
+                zt = zpool.tile([P, 2, CH], F32, tag="zt")
+                plain_stage(j, n, aT, zfi, zt)
+                if n == 0 and j + 1 < PAIRS:
+                    prep_m(j + 1)
+                    prep_last(j + 1)
+                mx_stage(j, n, zfi, zt)
+                finish(j, n, zfi, zt)
+                if n + 1 < NCH and j < 3:
+                    prep_weights(j, n + 1, False)
+                    if n + 3 < NCH:
+                        load_B(j, n + 3)
+                        load_A(j, n + 3)

@@ -24,6 +24,7 @@ NX = 256
 CH = 512
 NCH = MD // CH
 PAIRS = Q // 2
+VECTOR_TAIL = 14
 
 FLOPS = 2 * ROWS * MD * 3 * (UNITS + NX) + 2 * ROWS * UNITS * 6
 
@@ -35,7 +36,8 @@ def tile_edrncell_pa_kernel(
     with ExitStack() as ctx:
         const = ctx.enter_context(tc.tile_pool(name="const", bufs=1))
         raw = ctx.enter_context(tc.tile_pool(name="raw", bufs=6))
-        grp = ctx.enter_context(tc.tile_pool(name="grp", bufs=3))
+        grp = ctx.enter_context(tc.tile_pool(name="grp", bufs=2))
+        wgrp = ctx.enter_context(tc.tile_pool(name="wgrp", bufs=1))
         atp = ctx.enter_context(tc.tile_pool(name="atp", bufs=3))
         zpool = ctx.enter_context(tc.tile_pool(name="zpool", bufs=4))
         psum_y = ctx.enter_context(tc.psum_pool(name="psum_y", bufs=3))
@@ -48,6 +50,7 @@ def tile_edrncell_pa_kernel(
         out_v = out.rearrange("(p q) c -> p q c", q=Q)
         A_v = [w.rearrange("(t p) c -> p t c", p=P) for w in (A_fg, A_in, A_th)]
         B_v = [w.rearrange("(k p) c -> p k c", p=P) for w in (B_fg, B_in, B_th)]
+        b_v = [b.rearrange("o n -> (o n)") for b in (b_fg, b_in, b_th)]
 
         ident = const.tile([P, P], BF16)
         x_raw = const.tile([P, Q, NX], BF16)
@@ -59,21 +62,18 @@ def tile_edrncell_pa_kernel(
         l_codes = [const.tile([P, 2 * P], U32, name="l_codes%d" % j, align_bytes=64) for j in range(PAIRS)]
         l_scales = [const.tile([P, 2 * P], U8, name="l_scales%d" % j, align_bytes=64) for j in range(PAIRS)]
         B_sb = [[const.tile([P, 2, CH], BF16, name="B_sb%d_%d" % (g, n)) for n in range(NCH)] for g in range(3)]
-        A_codes = [
-            [const.tile([P, CH], U32, name="A_codes%d_%d" % (g, n), align_bytes=64) for n in range(NCH)]
-            for g in range(3)
-        ]
-        A_scales = [
-            [const.tile([P, CH], U8, name="A_scales%d_%d" % (g, n), align_bytes=64) for n in range(NCH)]
-            for g in range(3)
-        ]
-        bb = [const.tile([P, MD], BF16, name="bb%d" % g) for g in range(2)]
+        fi_codes = [const.tile([P, 2 * CH], U32, name="fi_codes%d" % n, align_bytes=64) for n in range(NCH)]
+        fi_scales = [const.tile([P, 2 * CH], U8, name="fi_scales%d" % n, align_bytes=64) for n in range(NCH)]
+        t_codes = [const.tile([P, CH], U32, name="t_codes%d" % n, align_bytes=64) for n in range(NCH)]
+        t_scales = [const.tile([P, CH], U8, name="t_scales%d" % n, align_bytes=64) for n in range(NCH)]
+        bb = [[const.tile([P, CH], BF16, name="bb%d_%d" % (g, n)) for n in range(NCH)] for g in range(2)]
         pt_raw = const.tile([P, 16, SLOTS], BF16)
         pt_msk = const.tile([P, 16, SLOTS], F32)
         p_blk = const.tile([P, 16, P], BF16)
-        b_row = const.tile([P, 16, P], BF16)
+        b_all = const.tile([P, 16, P], BF16)
         onehot = const.tile([P, SLOTS], F32)
         tri = const.tile([P, SLOTS], F32)
+        row3 = const.tile([P, 1], F32)
         same_unit = const.tile([P, P // SLOTS], F32)
         off_diag = const.tile([P, CH], BF16)
 
@@ -81,6 +81,9 @@ def tile_edrncell_pa_kernel(
 
         def load_B(g, n):
             nc.sync.dma_start(out=B_sb[g][n][:], in_=B_v[g][:, :, n * CH : (n + 1) * CH])
+
+        def load_bias(g, n):
+            nc.sync.dma_start(out=bb[g][n][:], in_=b_v[g][n * CH : (n + 1) * CH].partition_broadcast(P))
 
         def load_A(g, n):
             a_raw = raw.tile([P, 4, CH], BF16, tag="a_raw")
@@ -94,29 +97,27 @@ def tile_edrncell_pa_kernel(
             nc.sync.dma_start(out=a_sb[j][:], in_=a_v[:, 2 * j : 2 * j + 2, :])
 
         make_identity(nc, ident[:])
-        nc.vector.memset(b_row[:], 0.0)
-        nc.scalar.dma_start(out=b_row[3:4, :, :], in_=b_th.rearrange("o (c i) -> o c i", i=P))
         nc.scalar.dma_start(out=pt_raw[:], in_=A_pt_blk.rearrange("(c j) s t -> (j s) c t", j=P // SLOTS))
-        nc.scalar.dma_start(out=bb[0][:], in_=b_fg.rearrange("o n -> (o n)").partition_broadcast(P))
-        nc.scalar.dma_start(out=bb[1][:], in_=b_in.rearrange("o n -> (o n)").partition_broadcast(P))
         nc.sync.dma_start(out=x_raw[:], in_=x_v)
-        for g in range(3):
+        for g in range(2):
             load_B(g, 0)
+            load_bias(g, 0)
         load_m(0)
         load_A(0, 0)
         load_A(1, 0)
         load_a(0)
+        load_B(2, 0)
+        nc.sync.dma_start(out=b_all[:].rearrange("p c i -> p (c i)"), in_=b_v[2].partition_broadcast(P))
         load_A(2, 0)
-        load_m(1)
-        load_a(1)
-        for g in range(3):
-            load_B(g, 1)
+        for j in range(1, PAIRS):
+            load_m(j)
+            load_a(j)
         for g in range(3):
             load_A(g, 1)
-        load_m(2)
-        load_a(2)
-        load_m(3)
-        load_a(3)
+        for g in range(3):
+            load_B(g, 1)
+        for g in range(2):
+            load_bias(g, 1)
 
         nc.vector.tensor_reduce(
             out=onehot[:], in_=ident[:].rearrange("p (j s) -> p s j", s=SLOTS), axis=AXIS_X, op=ADD
@@ -128,6 +129,7 @@ def tile_edrncell_pa_kernel(
         nc.vector.tensor_copy(out=tri[:, 1:2], in_=onehot[:, 0:1])
         nc.vector.tensor_tensor(out=tri[:, 2:3], in0=tri[:, 1:2], in1=onehot[:, 1:2], op=ADD)
         nc.vector.tensor_tensor(out=tri[:, 3:4], in0=tri[:, 2:3], in1=onehot[:, 2:3], op=ADD)
+        nc.vector.tensor_copy(out=row3[:], in_=ident[:, 3:4])
         keep = tri[:, 3:4]
         one3 = onehot[:, 3:4]
         nc.vector.tensor_scalar(
@@ -148,7 +150,8 @@ def tile_edrncell_pa_kernel(
                 in1=same_unit[:].unsqueeze(1).to_broadcast([P, 16, P // SLOTS]),
                 op=MULT,
             )
-        nc.vector.tensor_tensor(out=p_blk[:], in0=p_blk[:], in1=b_row[:], op=ADD)
+        nc.vector.tensor_scalar(out=b_all[:], in0=b_all[:], scalar1=row3[:, 0:1], scalar2=None, op0=MULT)
+        nc.vector.tensor_tensor(out=p_blk[:], in0=p_blk[:], in1=b_all[:], op=ADD)
 
         for h in range(2):
             tp = psum_t.tile([P, 4, 2, P], BF16, tag="tp")
@@ -181,21 +184,32 @@ def tile_edrncell_pa_kernel(
                 l_scales,
             )
 
-        def prep_weights(g, n, on_vector):
-            a_raw = A_raw[(g, n)]
-            if g == 2:
-                nc.vector.tensor_tensor(out=a_raw[:, n, :], in0=a_raw[:, n, :], in1=off_diag[:], op=MULT)
-            a_grp = grp.tile([P, CH, 4], BF16, tag="a_grp", align_bytes=64)
-            dst = a_grp[:].rearrange("p (c i) t -> p c t i", i=4)
-            src = a_raw[:].rearrange("p t (c i) -> p c t i", i=4)
-            if on_vector:
-                nc.vector.tensor_copy(out=dst, in_=src)
-            else:
-                nc.scalar.copy(out=dst, in_=src)
+        def regroup(engine_copy, dst_tile, a_raw):
+            engine_copy(
+                out=dst_tile.rearrange("p (c i) t -> p c t i", i=4),
+                in_=a_raw[:].rearrange("p t (c i) -> p c t i", i=4),
+            )
+
+        def prep_fi(n):
+            fi_grp = wgrp.tile([P, 2, CH, 4], BF16, tag="fi_grp", align_bytes=64)
+            for g in range(2):
+                regroup(nc.scalar.copy, fi_grp[:, g, :, :], A_raw[(g, n)])
             nc.vector.quantize_mx(
-                out=A_codes[g][n][:].bitcast(FP8X4),
-                scales=A_scales[g][n][:],
-                in_=a_grp[:].rearrange("p w t -> p (w t)"),
+                out=fi_codes[n][:].bitcast(FP8X4),
+                scales=fi_scales[n][:],
+                in_=fi_grp[:].rearrange("p g w t -> p (g w t)"),
+            )
+
+        def prep_t(n):
+            a_raw = A_raw[(2, n)]
+            masker = nc.vector if n == 0 else nc.gpsimd
+            masker.tensor_tensor(out=a_raw[:, n, :], in0=a_raw[:, n, :], in1=off_diag[:], op=MULT)
+            t_grp = wgrp.tile([P, CH, 4], BF16, tag="t_grp", align_bytes=64)
+            regroup(nc.vector.tensor_copy if n == 0 else nc.scalar.copy, t_grp[:], a_raw)
+            nc.vector.quantize_mx(
+                out=t_codes[n][:].bitcast(FP8X4),
+                scales=t_scales[n][:],
+                in_=t_grp[:].rearrange("p w t -> p (w t)"),
             )
 
         def transpose_a(j, n):
@@ -216,9 +230,7 @@ def tile_edrncell_pa_kernel(
                     y = psum_y.tile([P, CH], F32, tag="y")
                     nc.tensor.matmul(y[:], lhsT=lhs[0], rhs=B_sb[g][n][:, 0, :], start=True, stop=False)
                     nc.tensor.matmul(y[:], lhsT=lhs[1], rhs=B_sb[g][n][:, 1, :], start=False, stop=True)
-                    nc.vector.tensor_tensor(
-                        out=zfi[:, g, qq, :], in0=y[:], in1=bb[g][:, n * CH : (n + 1) * CH], op=ADD
-                    )
+                    nc.vector.tensor_tensor(out=zfi[:, g, qq, :], in0=y[:], in1=bb[g][n][:], op=ADD)
                 y = psum_y.tile([P, CH], F32, tag="y")
                 nc.tensor.matmul(y[:], lhsT=lhs[0], rhs=B_sb[2][n][:, 0, :], start=True, stop=False)
                 for cb in range(4):
@@ -236,17 +248,28 @@ def tile_edrncell_pa_kernel(
             for qq in range(2):
                 rows = slice(qq * P, (qq + 1) * P)
                 for g in range(3):
-                    codes, scales = (m_codes, m_scales) if g < 2 else (l_codes, l_scales)
                     acc = psum_x.tile([P, CH], F32, tag="acc")
-                    nc.tensor.matmul_mx(
-                        out=acc[:],
-                        lhsT=codes[j][:, rows].bitcast(FP8X4),
-                        lhsT_scale=scales[j][:, rows],
-                        rhs=A_codes[g][n][:].bitcast(FP8X4),
-                        rhs_scale=A_scales[g][n][:],
-                        start=True,
-                        stop=True,
-                    )
+                    if g < 2:
+                        cols = slice(g * CH, (g + 1) * CH)
+                        nc.tensor.matmul_mx(
+                            out=acc[:],
+                            lhsT=m_codes[j][:, rows].bitcast(FP8X4),
+                            lhsT_scale=m_scales[j][:, rows],
+                            rhs=fi_codes[n][:, cols].bitcast(FP8X4),
+                            rhs_scale=fi_scales[n][:, cols],
+                            start=True,
+                            stop=True,
+                        )
+                    else:
+                        nc.tensor.matmul_mx(
+                            out=acc[:],
+                            lhsT=l_codes[j][:, rows].bitcast(FP8X4),
+                            lhsT_scale=l_scales[j][:, rows],
+                            rhs=t_codes[n][:].bitcast(FP8X4),
+                            rhs_scale=t_scales[n][:],
+                            start=True,
+                            stop=True,
+                        )
                     z = zfi[:, g, qq, :] if g < 2 else zt[:, qq, :]
                     nc.vector.tensor_tensor(out=z, in0=acc[:], in1=z, op=ADD)
 
@@ -254,22 +277,28 @@ def tile_edrncell_pa_kernel(
             nc.scalar.activation(out=zfi[:], in_=zfi[:], func=SIGMOID)
             nc.scalar.activation(out=zt[:], in_=zt[:], func=TANH)
             cols = slice(n * CH, (n + 1) * CH)
-            u = n * PAIRS + j
-            eng = nc.vector if (u % 5 == 0 and u > 0) else nc.gpsimd
+            eng = nc.vector if n * PAIRS + j >= VECTOR_TAIL else nc.gpsimd
             eng.tensor_tensor(out=zfi[:, 0, :, :], in0=zfi[:, 0, :, :], in1=a_sb[j][:, :, cols], op=MULT)
             eng.tensor_tensor(out=zt[:], in0=zt[:], in1=zfi[:, 1, :, :], op=MULT)
             eng.tensor_tensor(out=zfi[:, 0, :, :], in0=zfi[:, 0, :, :], in1=zt[:], op=ADD)
             nc.sync.dma_start(out=out_v[:, 2 * j : 2 * j + 2, cols], in_=zfi[:, 0, :, :])
 
+        def load_chunk(n):
+            for g in range(3):
+                load_A(g, n)
+            for g in range(3):
+                load_B(g, n)
+            for g in range(2):
+                load_bias(g, n)
+
         prep_m(0)
-        prep_weights(0, 0, True)
-        prep_weights(1, 0, True)
+        prep_fi(0)
         prep_last(0)
-        prep_weights(2, 0, True)
-        for g in range(3):
-            load_B(g, 2)
-        for g in range(3):
-            load_A(g, 2)
+        prep_t(0)
+        load_chunk(2)
+        for j in range(1, PAIRS):
+            prep_m(j)
+            prep_last(j)
 
         for n in range(NCH):
             for j in range(PAIRS):
@@ -277,13 +306,11 @@ def tile_edrncell_pa_kernel(
                 zfi = zpool.tile([P, 2, 2, CH], F32, tag="zfi")
                 zt = zpool.tile([P, 2, CH], F32, tag="zt")
                 plain_stage(j, n, aT, zfi, zt)
-                if n == 0 and j + 1 < PAIRS:
-                    prep_m(j + 1)
-                    prep_last(j + 1)
                 mx_stage(j, n, zfi, zt)
                 finish(j, n, zfi, zt)
-                if n + 1 < NCH and j < 3:
-                    prep_weights(j, n + 1, False)
+                if n + 1 < NCH and j == 0:
+                    prep_fi(n + 1)
+                if n + 1 < NCH and j == 1:
+                    prep_t(n + 1)
                     if n + 3 < NCH:
-                        load_B(j, n + 3)
-                        load_A(j, n + 3)
+                        load_chunk(n + 3)

@@ -17,14 +17,20 @@ AXIS_X = mybir.AxisListType.X
 P = 128
 ROWS = 1024
 Q = ROWS // P
+HALVES = 2
+QH = Q // HALVES
 UNITS = 512
 SLOTS = 4
 MD = UNITS * SLOTS
 NX = 256
 CH = 512
 NCH = MD // CH
+CB = CH // P
 PAIRS = Q // 2
-VECTOR_TAIL = 14
+UNITS_ALL = NCH * HALVES * CB
+ZBUFS = {1: 8, 2: 6}
+AHEAD = 4
+PLAIN_TH, MX_TH, TANH_LAG, BACK = 2, 3, 4, 7
 
 FLOPS = 2 * ROWS * MD * 3 * (UNITS + NX) + 2 * ROWS * UNITS * 6
 
@@ -34,15 +40,18 @@ def tile_edrncell_pa_kernel(
 ):
     nc = tc.nc
     with ExitStack() as ctx:
+        ctx.enter_context(tc.manual_schedule())
         const = ctx.enter_context(tc.tile_pool(name="const", bufs=1))
         raw = ctx.enter_context(tc.tile_pool(name="raw", bufs=6))
-        grp = ctx.enter_context(tc.tile_pool(name="grp", bufs=2))
+        grp = ctx.enter_context(tc.tile_pool(name="grp", bufs=4))
         wgrp = ctx.enter_context(tc.tile_pool(name="wgrp", bufs=1))
-        atp = ctx.enter_context(tc.tile_pool(name="atp", bufs=3))
-        zpool = ctx.enter_context(tc.tile_pool(name="zpool", bufs=4))
+        atp = ctx.enter_context(tc.tile_pool(name="atp", bufs=2))
+        fpool = ctx.enter_context(tc.tile_pool(name="fpool", bufs=4))
+        tpool = ctx.enter_context(tc.tile_pool(name="tpool", bufs=5))
         psum_y = ctx.enter_context(tc.psum_pool(name="psum_y", bufs=3))
-        psum_x = ctx.enter_context(tc.psum_pool(name="psum_x", bufs=3))
+        psum_x = ctx.enter_context(tc.psum_pool(name="psum_x", bufs=2))
         psum_t = ctx.enter_context(tc.psum_pool(name="psum_t", bufs=2))
+        psum_o = ctx.enter_context(tc.psum_pool(name="psum_o", bufs=1))
 
         x_v = x_t.rearrange("(p q) k -> p q k", q=Q)
         m_v = m_t.rearrange("(p q) k -> p q k", q=Q)
@@ -50,30 +59,32 @@ def tile_edrncell_pa_kernel(
         out_v = out.rearrange("(p q) c -> p q c", q=Q)
         A_v = [w.rearrange("(t p) c -> p t c", p=P) for w in (A_fg, A_in, A_th)]
         B_v = [w.rearrange("(k p) c -> p k c", p=P) for w in (B_fg, B_in, B_th)]
-        b_v = [b.rearrange("o n -> (o n)") for b in (b_fg, b_in, b_th)]
 
         ident = const.tile([P, P], BF16)
+        ident_f = const.tile([P, P], F32)
         x_raw = const.tile([P, Q, NX], BF16)
         m_raw = [const.tile([P, 2, UNITS], BF16, name="m_raw%d" % j) for j in range(PAIRS)]
         a_sb = [const.tile([P, 2, MD], BF16, name="a_sb%d" % j) for j in range(PAIRS)]
-        xT = [const.tile([P, 4, 2, P], BF16, name="xT%d" % h) for h in range(2)]
-        m_codes = [const.tile([P, 2 * P], U32, name="m_codes%d" % j, align_bytes=64) for j in range(PAIRS)]
-        m_scales = [const.tile([P, 2 * P], U8, name="m_scales%d" % j, align_bytes=64) for j in range(PAIRS)]
-        l_codes = [const.tile([P, 2 * P], U32, name="l_codes%d" % j, align_bytes=64) for j in range(PAIRS)]
-        l_scales = [const.tile([P, 2 * P], U8, name="l_scales%d" % j, align_bytes=64) for j in range(PAIRS)]
+        xT = [const.tile([P, 2, QH, P], BF16, name="xT%d" % h) for h in range(HALVES)]
+        m_codes = [const.tile([P, QH * P], U32, name="m_codes%d" % h, align_bytes=64) for h in range(HALVES)]
+        m_scales = [const.tile([P, QH * P], U8, name="m_scales%d" % h, align_bytes=64) for h in range(HALVES)]
+        l_codes = [const.tile([P, QH * P], U32, name="l_codes%d" % h, align_bytes=64) for h in range(HALVES)]
+        l_scales = [const.tile([P, QH * P], U8, name="l_scales%d" % h, align_bytes=64) for h in range(HALVES)]
         B_sb = [[const.tile([P, 2, CH], BF16, name="B_sb%d_%d" % (g, n)) for n in range(NCH)] for g in range(3)]
-        fi_codes = [const.tile([P, 2 * CH], U32, name="fi_codes%d" % n, align_bytes=64) for n in range(NCH)]
-        fi_scales = [const.tile([P, 2 * CH], U8, name="fi_scales%d" % n, align_bytes=64) for n in range(NCH)]
-        t_codes = [const.tile([P, CH], U32, name="t_codes%d" % n, align_bytes=64) for n in range(NCH)]
-        t_scales = [const.tile([P, CH], U8, name="t_scales%d" % n, align_bytes=64) for n in range(NCH)]
-        bb = [[const.tile([P, CH], BF16, name="bb%d_%d" % (g, n)) for n in range(NCH)] for g in range(2)]
+        A_codes = [
+            [const.tile([P, CH], U32, name="A_codes%d_%d" % (g, n), align_bytes=64) for n in range(NCH)] for g in range(3)
+        ]
+        A_scales = [
+            [const.tile([P, CH], U8, name="A_scales%d_%d" % (g, n), align_bytes=64) for n in range(NCH)] for g in range(3)
+        ]
+        bb = [const.tile([P, CH], BF16, name="bb%d" % n) for n in range(NCH)]
+        b_rows = const.tile([P, P], BF16)
+        b_cols = const.tile([P, 2, NCH, CB], F32)
         pt_raw = const.tile([P, 16, SLOTS], BF16)
         pt_msk = const.tile([P, 16, SLOTS], F32)
         p_blk = const.tile([P, 16, P], BF16)
-        b_all = const.tile([P, 16, P], BF16)
         onehot = const.tile([P, SLOTS], F32)
         tri = const.tile([P, SLOTS], F32)
-        row3 = const.tile([P, 1], F32)
         same_unit = const.tile([P, P // SLOTS], F32)
         off_diag = const.tile([P, CH], BF16)
 
@@ -82,8 +93,10 @@ def tile_edrncell_pa_kernel(
         def load_B(g, n):
             nc.sync.dma_start(out=B_sb[g][n][:], in_=B_v[g][:, :, n * CH : (n + 1) * CH])
 
-        def load_bias(g, n):
-            nc.sync.dma_start(out=bb[g][n][:], in_=b_v[g][n * CH : (n + 1) * CH].partition_broadcast(P))
+        def load_bias(n):
+            nc.sync.dma_start(
+                out=bb[n][:], in_=b_fg.rearrange("o n -> (o n)")[n * CH : (n + 1) * CH].partition_broadcast(P)
+            )
 
         def load_A(g, n):
             a_raw = raw.tile([P, 4, CH], BF16, tag="a_raw")
@@ -97,27 +110,32 @@ def tile_edrncell_pa_kernel(
             nc.sync.dma_start(out=a_sb[j][:], in_=a_v[:, 2 * j : 2 * j + 2, :])
 
         make_identity(nc, ident[:])
+        make_identity(nc, ident_f[:])
         nc.scalar.dma_start(out=pt_raw[:], in_=A_pt_blk.rearrange("(c j) s t -> (j s) c t", j=P // SLOTS))
+        nc.vector.memset(b_rows[:], 0.0)
+        for g, b in enumerate((b_in, b_th)):
+            nc.scalar.dma_start(out=b_rows[16 * g : 16 * g + 16, :], in_=b.rearrange("o (c p) -> (o c) p", p=P))
         nc.sync.dma_start(out=x_raw[:], in_=x_v)
-        for g in range(2):
-            load_B(g, 0)
-            load_bias(g, 0)
-        load_m(0)
+        load_B(0, 0)
+        load_bias(0)
+        load_B(1, 0)
         load_A(0, 0)
+        load_m(0)
         load_A(1, 0)
+        load_m(1)
         load_a(0)
-        load_B(2, 0)
-        nc.sync.dma_start(out=b_all[:].rearrange("p c i -> p (c i)"), in_=b_v[2].partition_broadcast(P))
         load_A(2, 0)
-        for j in range(1, PAIRS):
+        load_a(1)
+        load_B(2, 0)
+        for j in range(2, PAIRS):
             load_m(j)
+        for j in range(2, PAIRS):
             load_a(j)
         for g in range(3):
             load_A(g, 1)
         for g in range(3):
             load_B(g, 1)
-        for g in range(2):
-            load_bias(g, 1)
+        load_bias(1)
 
         nc.vector.tensor_reduce(
             out=onehot[:], in_=ident[:].rearrange("p (j s) -> p s j", s=SLOTS), axis=AXIS_X, op=ADD
@@ -129,10 +147,7 @@ def tile_edrncell_pa_kernel(
         nc.vector.tensor_copy(out=tri[:, 1:2], in_=onehot[:, 0:1])
         nc.vector.tensor_tensor(out=tri[:, 2:3], in0=tri[:, 1:2], in1=onehot[:, 1:2], op=ADD)
         nc.vector.tensor_tensor(out=tri[:, 3:4], in0=tri[:, 2:3], in1=onehot[:, 2:3], op=ADD)
-        nc.vector.tensor_copy(out=row3[:], in_=ident[:, 3:4])
-        keep = tri[:, 3:4]
-        one3 = onehot[:, 3:4]
-        nc.vector.tensor_scalar(
+        nc.gpsimd.tensor_scalar(
             out=off_diag[:].rearrange("p (i s) -> p i s", s=SLOTS),
             in0=ident[:].unsqueeze(2).to_broadcast([P, P, SLOTS]),
             scalar1=-1.0,
@@ -143,174 +158,284 @@ def tile_edrncell_pa_kernel(
         nc.vector.tensor_tensor(
             out=pt_msk[:], in0=pt_raw[:], in1=tri[:].unsqueeze(1).to_broadcast([P, 16, SLOTS]), op=MULT
         )
-        for t in range(SLOTS):
-            nc.vector.tensor_tensor(
-                out=p_blk[:].rearrange("p c (j t) -> p c j t", t=SLOTS)[:, :, :, t],
-                in0=pt_msk[:, :, t : t + 1].to_broadcast([P, 16, P // SLOTS]),
-                in1=same_unit[:].unsqueeze(1).to_broadcast([P, 16, P // SLOTS]),
+        block = [P, 4, P // SLOTS, SLOTS]
+        for n in range(NCH):
+            part = slice(4 * n, 4 * n + 4)
+            nc.gpsimd.tensor_tensor(
+                out=p_blk[:, part, :].rearrange("p c (j t) -> p c j t", t=SLOTS),
+                in0=pt_msk[:, part, :].unsqueeze(2).to_broadcast(block),
+                in1=same_unit[:].unsqueeze(1).unsqueeze(3).to_broadcast(block),
                 op=MULT,
             )
-        nc.vector.tensor_scalar(out=b_all[:], in0=b_all[:], scalar1=row3[:, 0:1], scalar2=None, op0=MULT)
-        nc.vector.tensor_tensor(out=p_blk[:], in0=p_blk[:], in1=b_all[:], op=ADD)
 
-        for h in range(2):
-            tp = psum_t.tile([P, 4, 2, P], BF16, tag="tp")
-            for qh in range(4):
-                for k in range(2):
-                    nc.tensor.transpose(tp[:, qh, k, :], x_raw[:, 4 * h + qh, k * P : (k + 1) * P], ident[:])
-            nc.scalar.copy(out=xT[h][:], in_=tp[:])
+        def transpose_x(h, engine_copy):
+            tp = psum_t.tile([P, 2, QH, P], BF16, tag="tp")
+            for k in range(2):
+                for r in range(QH):
+                    nc.tensor.transpose(tp[:, k, r, :], x_raw[:, QH * h + r, k * P : (k + 1) * P], ident[:])
+            engine_copy(out=xT[h][:], in_=tp[:])
 
-        def quantise_rows(j, source, codes, scales):
+        def transpose_bias():
+            tp = psum_t.tile([P, P], BF16, tag="tp")
+            nc.tensor.transpose(tp[:], b_rows[:], ident[:])
+            nc.vector.tensor_copy(
+                out=b_cols[:].rearrange("p g n c -> p (g n c)"), in_=tp[:, 0 : 2 * NCH * CB]
+            )
+
+        def rows_to_k(raw_tile, view, engine_copy):
             tp = psum_t.tile([P, 2, 4, P], BF16, tag="tp")
             for qq in range(2):
                 for t in range(4):
-                    nc.tensor.transpose(tp[:, qq, t, :], source(qq, t), ident[:])
+                    nc.tensor.transpose(tp[:, qq, t, :], view(raw_tile, qq, t), ident[:])
             g4 = grp.tile([P, 2, P, 4], BF16, tag="g4", align_bytes=64)
-            nc.scalar.copy(out=g4[:], in_=tp[:].rearrange("p q t b -> p q b t"))
+            engine_copy(out=g4[:], in_=tp[:].rearrange("p q t b -> p q b t"))
+            return g4
+
+        def of_m(j):
+            return m_raw[j], lambda tile, qq, t: tile[:, qq, t * P : (t + 1) * P]
+
+        def of_last(j):
+            return a_sb[j], lambda tile, qq, t: tile[:, qq, :].rearrange("p (t i s) -> p t i s", t=4, s=SLOTS)[:, t, :, 3]
+
+        def quantise_rows(j, g4, codes, scales):
+            h, cols = j // 2, slice(j % 2 * 2 * P, (j % 2 + 1) * 2 * P)
             nc.vector.quantize_mx(
-                out=codes[j][:].bitcast(FP8X4),
-                scales=scales[j][:],
+                out=codes[h][:, cols].bitcast(FP8X4),
+                scales=scales[h][:, cols],
                 in_=g4[:].rearrange("p q b t -> p (q b t)"),
             )
 
-        def prep_m(j):
-            quantise_rows(j, lambda qq, t: m_raw[j][:, qq, t * P : (t + 1) * P], m_codes, m_scales)
+        grouped = {}
 
-        def prep_last(j):
-            quantise_rows(
-                j,
-                lambda qq, t: a_sb[j][:, qq, :].rearrange("p (t i s) -> p t i s", t=4, s=SLOTS)[:, t, :, 3],
-                l_codes,
-                l_scales,
-            )
-
-        def regroup(engine_copy, dst_tile, a_raw):
-            engine_copy(
-                out=dst_tile.rearrange("p (c i) t -> p c t i", i=4),
-                in_=a_raw[:].rearrange("p t (c i) -> p c t i", i=4),
-            )
-
-        def prep_fi(n):
-            fi_grp = wgrp.tile([P, 2, CH, 4], BF16, tag="fi_grp", align_bytes=64)
-            for g in range(2):
-                regroup(nc.scalar.copy, fi_grp[:, g, :, :], A_raw[(g, n)])
-            nc.vector.quantize_mx(
-                out=fi_codes[n][:].bitcast(FP8X4),
-                scales=fi_scales[n][:],
-                in_=fi_grp[:].rearrange("p g w t -> p (g w t)"),
-            )
-
-        def prep_t(n):
+        def mask_A_th(n):
             a_raw = A_raw[(2, n)]
-            masker = nc.vector if n == 0 else nc.gpsimd
-            masker.tensor_tensor(out=a_raw[:, n, :], in0=a_raw[:, n, :], in1=off_diag[:], op=MULT)
-            t_grp = wgrp.tile([P, CH, 4], BF16, tag="t_grp", align_bytes=64)
-            regroup(nc.vector.tensor_copy if n == 0 else nc.scalar.copy, t_grp[:], a_raw)
+            nc.gpsimd.tensor_tensor(out=a_raw[:, n, :], in0=a_raw[:, n, :], in1=off_diag[:], op=MULT)
+
+        def regroup(g, n, quarter=None):
+            if (g, n) not in grouped:
+                grouped[(g, n)] = wgrp.tile([P, CH, 4], BF16, name="grouped", tag="grouped%d" % g, align_bytes=64)
+            if quarter is not None:
+                spans = [(nc.scalar.copy, quarter * P, (quarter + 1) * P)]
+            elif n == 0:
+                spans = [(nc.vector.tensor_copy, 0, CH // 2), (nc.scalar.copy, CH // 2, CH)]
+            else:
+                spans = [(None, 0, CH)]
+            for engine_copy, lo, hi in spans:
+                dst = grouped[(g, n)][:, lo:hi, :].rearrange("p (c i) t -> p c t i", i=4)
+                src = A_raw[(g, n)][:, :, lo:hi].rearrange("p t (c i) -> p c t i", i=4)
+                if engine_copy is None:
+                    nc.gpsimd.tensor_scalar(out=dst, in0=src, scalar1=1.0, scalar2=0.0, op0=MULT, op1=ADD)
+                else:
+                    engine_copy(out=dst, in_=src)
+
+        def quantise_A(g, n):
             nc.vector.quantize_mx(
-                out=t_codes[n][:].bitcast(FP8X4),
-                scales=t_scales[n][:],
-                in_=t_grp[:].rearrange("p w t -> p (w t)"),
+                out=A_codes[g][n][:].bitcast(FP8X4),
+                scales=A_scales[g][n][:],
+                in_=grouped[(g, n)][:].rearrange("p w t -> p (w t)"),
             )
-
-        def transpose_a(j, n):
-            tp = psum_t.tile([P, 2, 4, P], BF16, tag="tp")
-            for qq in range(2):
-                for cb in range(4):
-                    c = 4 * n + cb
-                    nc.tensor.transpose(tp[:, qq, cb, :], a_sb[j][:, qq, c * P : (c + 1) * P], ident[:])
-            aT = atp.tile([P, 2, 4, P], BF16, tag="aT")
-            nc.vector.tensor_scalar(out=aT[:], in0=tp[:], scalar1=keep, scalar2=one3, op0=MULT, op1=ADD)
-            return aT
-
-        def plain_stage(j, n, aT, zfi, zt):
-            for qq in range(2):
-                q = 2 * j + qq
-                lhs = [xT[q // 4][:, q % 4, k, :] for k in range(2)]
-                for g in range(2):
-                    y = psum_y.tile([P, CH], F32, tag="y")
-                    nc.tensor.matmul(y[:], lhsT=lhs[0], rhs=B_sb[g][n][:, 0, :], start=True, stop=False)
-                    nc.tensor.matmul(y[:], lhsT=lhs[1], rhs=B_sb[g][n][:, 1, :], start=False, stop=True)
-                    nc.vector.tensor_tensor(out=zfi[:, g, qq, :], in0=y[:], in1=bb[g][n][:], op=ADD)
-                y = psum_y.tile([P, CH], F32, tag="y")
-                nc.tensor.matmul(y[:], lhsT=lhs[0], rhs=B_sb[2][n][:, 0, :], start=True, stop=False)
-                for cb in range(4):
-                    nc.tensor.matmul(
-                        y[:, cb * P : (cb + 1) * P],
-                        lhsT=aT[:, qq, cb, :],
-                        rhs=p_blk[:, 4 * n + cb, :],
-                        start=False,
-                        stop=False,
-                    )
-                nc.tensor.matmul(y[:], lhsT=lhs[1], rhs=B_sb[2][n][:, 1, :], start=False, stop=True)
-                nc.scalar.copy(out=zt[:, qq, :], in_=y[:])
-
-        def mx_stage(j, n, zfi, zt):
-            for qq in range(2):
-                rows = slice(qq * P, (qq + 1) * P)
-                for g in range(3):
-                    acc = psum_x.tile([P, CH], F32, tag="acc")
-                    if g < 2:
-                        cols = slice(g * CH, (g + 1) * CH)
-                        nc.tensor.matmul_mx(
-                            out=acc[:],
-                            lhsT=m_codes[j][:, rows].bitcast(FP8X4),
-                            lhsT_scale=m_scales[j][:, rows],
-                            rhs=fi_codes[n][:, cols].bitcast(FP8X4),
-                            rhs_scale=fi_scales[n][:, cols],
-                            start=True,
-                            stop=True,
-                        )
-                    else:
-                        nc.tensor.matmul_mx(
-                            out=acc[:],
-                            lhsT=l_codes[j][:, rows].bitcast(FP8X4),
-                            lhsT_scale=l_scales[j][:, rows],
-                            rhs=t_codes[n][:].bitcast(FP8X4),
-                            rhs_scale=t_scales[n][:],
-                            start=True,
-                            stop=True,
-                        )
-                    z = zfi[:, g, qq, :] if g < 2 else zt[:, qq, :]
-                    nc.vector.tensor_tensor(out=z, in0=acc[:], in1=z, op=ADD)
-
-        def finish(j, n, zfi, zt):
-            nc.scalar.activation(out=zfi[:], in_=zfi[:], func=SIGMOID)
-            nc.scalar.activation(out=zt[:], in_=zt[:], func=TANH)
-            cols = slice(n * CH, (n + 1) * CH)
-            eng = nc.vector if n * PAIRS + j >= VECTOR_TAIL else nc.gpsimd
-            eng.tensor_tensor(out=zfi[:, 0, :, :], in0=zfi[:, 0, :, :], in1=a_sb[j][:, :, cols], op=MULT)
-            eng.tensor_tensor(out=zt[:], in0=zt[:], in1=zfi[:, 1, :, :], op=MULT)
-            eng.tensor_tensor(out=zfi[:, 0, :, :], in0=zfi[:, 0, :, :], in1=zt[:], op=ADD)
-            nc.sync.dma_start(out=out_v[:, 2 * j : 2 * j + 2, cols], in_=zfi[:, 0, :, :])
 
         def load_chunk(n):
             for g in range(3):
                 load_A(g, n)
             for g in range(3):
                 load_B(g, n)
-            for g in range(2):
-                load_bias(g, n)
+            load_bias(n)
 
-        prep_m(0)
-        prep_fi(0)
-        prep_last(0)
-        prep_t(0)
-        load_chunk(2)
-        for j in range(1, PAIRS):
-            prep_m(j)
-            prep_last(j)
+        zf, zg, aT = {}, {1: {}, 2: {}}, {}
 
-        for n in range(NCH):
-            for j in range(PAIRS):
-                aT = transpose_a(j, n)
-                zfi = zpool.tile([P, 2, 2, CH], F32, tag="zfi")
-                zt = zpool.tile([P, 2, CH], F32, tag="zt")
-                plain_stage(j, n, aT, zfi, zt)
-                mx_stage(j, n, zfi, zt)
-                finish(j, n, zfi, zt)
-                if n + 1 < NCH and j == 0:
-                    prep_fi(n + 1)
-                if n + 1 < NCH and j == 1:
-                    prep_t(n + 1)
-                    if n + 3 < NCH:
-                        load_chunk(n + 3)
+        def place(u):
+            return u // 8, u // 4 % 2, u % 4
+
+        def plain_fg(u):
+            n, h, s = place(u)
+            if s == 0:
+                zf[u // 4] = fpool.tile([P, QH, CH], F32, name="zf", tag="zf")
+            y = psum_y.tile([P, CH], F32, tag="y")
+            for k in range(2):
+                nc.tensor.matmul(y[:], lhsT=xT[h][:, k, s, :], rhs=B_sb[0][n][:, k, :], start=(k == 0), stop=(k == 1))
+            nc.vector.tensor_tensor(out=zf[u // 4][:, s, :], in0=y[:], in1=bb[n][:], op=ADD)
+
+        def mx_fg(u):
+            n, h, s = place(u)
+            rows = slice(s * P, (s + 1) * P)
+            acc = psum_x.tile([P, CH], F32, tag="acc")
+            nc.tensor.matmul_mx(
+                out=acc[:],
+                lhsT=m_codes[h][:, rows].bitcast(FP8X4),
+                lhsT_scale=m_scales[h][:, rows],
+                rhs=A_codes[0][n][:].bitcast(FP8X4),
+                rhs_scale=A_scales[0][n][:],
+                start=True,
+                stop=True,
+            )
+            z = zf[u // 4][:, s, :]
+            nc.vector.tensor_tensor(out=z, in0=acc[:], in1=z, op=ADD)
+
+        def sigmoid_fg(u):
+            z = zf[u // 4][:, u % 4, :]
+            nc.scalar.activation(out=z, in_=z, func=SIGMOID)
+
+        def product_fg(u):
+            n, h, s = place(u)
+            z = zf[u // 4][:, s - 1 : s + 1, :]
+            nc.gpsimd.tensor_tensor(
+                out=z, in0=z, in1=a_sb[2 * h + s // 2][:, :, n * CH : (n + 1) * CH], op=MULT
+            )
+
+        def plain_gate(u, g):
+            n, h, s = place(u)
+            cols = slice(s * P, (s + 1) * P)
+            zg[g][u] = tpool.tile([P, QH * P], F32, name="zg%d" % g, tag="zg%d" % g, bufs=ZBUFS[g])
+            y = psum_y.tile([P, QH * P], F32, tag="y")
+            x_k = [xT[h][:, k, :, :].rearrange("p r b -> p (r b)") for k in range(2)]
+            nc.tensor.matmul(y[:], lhsT=B_sb[g][n][:, 0, cols], rhs=x_k[0], start=True, stop=False)
+            nc.tensor.matmul(y[:], lhsT=B_sb[g][n][:, 1, cols], rhs=x_k[1], start=False, stop=(g == 1))
+            if g == 2:
+                nc.tensor.matmul(
+                    y[:],
+                    lhsT=p_blk[:, CB * n + s, :],
+                    rhs=aT[u // 4][:, s, :, :].rearrange("p r b -> p (r b)"),
+                    start=False,
+                    stop=True,
+                )
+            (nc.vector.tensor_copy if g == 1 and s == 3 else nc.scalar.copy)(out=gate_tile(u, g), in_=y[:])
+
+        def gate_tile(u, g):
+            return zg[g][u][:]
+
+        def mx_gate(u, g):
+            n, h, s = place(u)
+            cols = slice(s * P, (s + 1) * P)
+            acc = psum_x.tile([P, QH * P], F32, tag="acc")
+            codes, scales = (m_codes, m_scales) if g == 1 else (l_codes, l_scales)
+            nc.tensor.matmul_mx(
+                out=acc[:],
+                lhsT=A_codes[g][n][:, cols].bitcast(FP8X4),
+                lhsT_scale=A_scales[g][n][:, cols],
+                rhs=codes[h][:].bitcast(FP8X4),
+                rhs_scale=scales[h][:],
+                start=True,
+                stop=True,
+            )
+            z = gate_tile(u, g)
+            nc.vector.tensor_tensor(out=z, in0=acc[:], in1=z, op=ADD)
+
+        def activate_gate(u, g):
+            n, h, s = place(u)
+            z = gate_tile(u, g)
+            nc.scalar.activation(out=z, in_=z, func=SIGMOID if g == 1 else TANH, bias=b_cols[:, g - 1, n, s : s + 1])
+
+        def product_th(u):
+            z = gate_tile(u, 2)
+            nc.gpsimd.tensor_tensor(out=z, in0=z, in1=gate_tile(u, 1), op=MULT)
+
+        def turn_back(u):
+            back = psum_o.tile([P, QH, P], F32, name="back", tag="back")
+            for r in range(QH):
+                nc.tensor.transpose(back[:, r, :], gate_tile(u, 2)[:, r * P : (r + 1) * P], ident_f[:])
+            return back
+
+        def total(u, back):
+            n, h, s = place(u)
+            z = zf[u // 4][:, :, s * P : (s + 1) * P]
+            nc.vector.tensor_tensor(out=z, in0=back[:], in1=z, op=ADD)
+            width = P if u // 4 == UNITS_ALL // 4 - 1 else 2 * P
+            if (s + 1) * P % width == 0:
+                lo = (s + 1) * P - width
+                nc.sync.dma_start(
+                    out=out_v[:, QH * h : QH * (h + 1), n * CH + lo : n * CH + lo + width],
+                    in_=zf[u // 4][:, :, lo : lo + width],
+                )
+
+        def transpose_a(macro, part):
+            n, h = macro // 2, macro % 2
+            if part == 0:
+                aT[macro] = atp.tile([P, CB, QH, P], BF16, name="aT", tag="aT")
+            tp = psum_t.tile([P, 2, QH, P], BF16, tag="tp")
+            for c in range(2):
+                col = n * CH + (2 * part + c) * P
+                for r in range(QH):
+                    nc.tensor.transpose(tp[:, c, r, :], a_sb[2 * h + r // 2][:, r % 2, col : col + P], ident[:])
+            nc.scalar.copy(out=aT[macro][:, 2 * part : 2 * part + 2, :, :], in_=tp[:])
+
+        v_copy, s_copy = nc.vector.tensor_copy, nc.scalar.copy
+        transpose_x(0, v_copy)
+        plain_fg(0)
+        plain_gate(0, 1)
+        plain_fg(1)
+        plain_gate(1, 1)
+        transpose_bias()
+        plain_fg(2)
+        regroup(0, 0)
+        m0 = rows_to_k(*of_m(0), s_copy)
+        quantise_A(0, 0)
+        plain_gate(2, 1)
+        transpose_x(1, s_copy)
+        regroup(1, 0)
+        quantise_rows(0, m0, m_codes, m_scales)
+        m1 = rows_to_k(*of_m(1), v_copy)
+        quantise_A(1, 0)
+        plain_fg(3)
+        plain_gate(3, 1)
+        quantise_rows(1, m1, m_codes, m_scales)
+        mask_A_th(0)
+
+        row_tasks = {
+            1: [("l", 0), ("m", 2)],
+            2: [("l", 1), ("m", 3)],
+            4: [("l", 2)],
+            5: [("l", 3)],
+        }
+        pending = []
+        for t in range(UNITS_ALL + BACK):
+            if t < UNITS_ALL:
+                mx_fg(t)
+            if 0 <= t - 1 < UNITS_ALL:
+                sigmoid_fg(t - 1)
+                activate_gate(t - 1, 1)
+                if (t - 1) % 2:
+                    product_fg(t - 1)
+            if AHEAD <= t + 2 < UNITS_ALL:
+                plain_fg(t + 2)
+            if t < UNITS_ALL:
+                mx_gate(t, 1)
+            if 0 <= t - TANH_LAG < UNITS_ALL:
+                activate_gate(t - TANH_LAG, 2)
+                product_th(t - TANH_LAG)
+            if AHEAD <= t + 2 < UNITS_ALL:
+                plain_gate(t + 2, 1)
+            back = turn_back(t - BACK) if 0 <= t - BACK else None
+            if t % 2 == 1 and t // 4 < UNITS_ALL // 4:
+                transpose_a(t // 4, t % 4 // 2)
+            fresh = [(kind, j, rows_to_k(*(of_m(j) if kind == "m" else of_last(j)), v_copy)) for kind, j in row_tasks.get(t, ())]
+            if 0 <= t - PLAIN_TH < UNITS_ALL:
+                plain_gate(t - PLAIN_TH, 2)
+            for kind, j, g4 in pending:
+                codes, scales = (m_codes, m_scales) if kind == "m" else (l_codes, l_scales)
+                quantise_rows(j, g4, codes, scales)
+            pending = fresh
+            if back is not None:
+                total(t - BACK, back)
+            if 0 <= t - MX_TH < UNITS_ALL:
+                mx_gate(t - MX_TH, 2)
+            n, s8 = t // 8 + 1, t % 8
+            if t == 1:
+                regroup(2, 0)
+            if t == 2:
+                quantise_A(2, 0)
+                load_chunk(2)
+            if n < NCH:
+                if s8 == 1:
+                    mask_A_th(n)
+                if s8 == 2:
+                    regroup(2, n)
+                if 3 <= s8 < 7:
+                    regroup(0, n, s8 - 3)
+                    regroup(1, n, s8 - 3)
+                if s8 == 7:
+                    quantise_A(0, n)
+                    quantise_A(1, n)
+                    quantise_A(2, n)
+                    if n + 2 < NCH:
+                        load_chunk(n + 2)

@@ -29,6 +29,7 @@ CB = CH // P
 PAIRS = Q // 2
 UNITS_ALL = NCH * HALVES * CB
 ZBUFS = {1: 8, 2: 6}
+QUANT = {True: {6: (0,), 7: (2, 1)}, False: {3: (0,), 5: (2,), 6: (1,)}}
 AHEAD = 4
 PLAIN_TH, MX_TH, TANH_LAG, BACK = 2, 3, 4, 7
 
@@ -57,7 +58,8 @@ def tile_edrncell_pa_kernel(
         m_v = m_t.rearrange("(p q) k -> p q k", q=Q)
         a_v = a_t.rearrange("(p q) c -> p q c", q=Q)
         out_v = out.rearrange("(p q) c -> p q c", q=Q)
-        A_v = [w.rearrange("(t p) c -> p t c", p=P) for w in (A_fg, A_in, A_th)]
+        A_v = [w.rearrange("(p t) c -> p t c", p=P) for w in (A_fg, A_in)]
+        A_v.append(A_th.rearrange("(t p) c -> p t c", p=P))
         B_v = [w.rearrange("(k p) c -> p k c", p=P) for w in (B_fg, B_in, B_th)]
 
         ident = const.tile([P, P], BF16)
@@ -116,11 +118,11 @@ def tile_edrncell_pa_kernel(
         for g, b in enumerate((b_in, b_th)):
             nc.scalar.dma_start(out=b_rows[16 * g : 16 * g + 16, :], in_=b.rearrange("o (c p) -> (o c) p", p=P))
         nc.sync.dma_start(out=x_raw[:], in_=x_v)
+        load_A(0, 0)
         load_B(0, 0)
+        load_m(0)
         load_bias(0)
         load_B(1, 0)
-        load_A(0, 0)
-        load_m(0)
         load_A(1, 0)
         load_m(1)
         load_a(0)
@@ -182,6 +184,22 @@ def tile_edrncell_pa_kernel(
                 out=b_cols[:].rearrange("p g n c -> p (g n c)"), in_=tp[:, 0 : 2 * NCH * CB]
             )
 
+        def m_to_k(j, engine_copy):
+            words = m_raw[j][:].bitcast(F32)
+            tp = psum_t.tile([P, 2, 2, P], F32, tag="tp")
+            for qq in range(2):
+                for w in range(2):
+                    nc.tensor.transpose(tp[:, qq, w, :], words[:, qq, w : UNITS // 2 : 2], ident_f[:])
+            g4 = grp.tile([P, 2, P, 4], BF16, tag="g4", align_bytes=64)
+            engine_copy(
+                out=g4[:].rearrange("p q b t -> p (q b t)").bitcast(F32).rearrange("p (q b w) -> p q b w", q=2, w=2),
+                in_=tp[:].rearrange("p q w b -> p q b w"),
+            )
+            return g4
+
+        def last_to_k(j, engine_copy):
+            return rows_to_k(*of_last(j), engine_copy)
+
         def rows_to_k(raw_tile, view, engine_copy):
             tp = psum_t.tile([P, 2, 4, P], BF16, tag="tp")
             for qq in range(2):
@@ -190,9 +208,6 @@ def tile_edrncell_pa_kernel(
             g4 = grp.tile([P, 2, P, 4], BF16, tag="g4", align_bytes=64)
             engine_copy(out=g4[:], in_=tp[:].rearrange("p q t b -> p q b t"))
             return g4
-
-        def of_m(j):
-            return m_raw[j], lambda tile, qq, t: tile[:, qq, t * P : (t + 1) * P]
 
         def of_last(j):
             return a_sb[j], lambda tile, qq, t: tile[:, qq, :].rearrange("p (t i s) -> p t i s", t=4, s=SLOTS)[:, t, :, 3]
@@ -216,7 +231,7 @@ def tile_edrncell_pa_kernel(
                 grouped[(g, n)] = wgrp.tile([P, CH, 4], BF16, name="grouped", tag="grouped%d" % g, align_bytes=64)
             if quarter is not None:
                 spans = [(nc.scalar.copy, quarter * P, (quarter + 1) * P)]
-            elif n == 0:
+            elif n == 0 and g < 2:
                 spans = [(nc.vector.tensor_copy, 0, CH // 2), (nc.scalar.copy, CH // 2, CH)]
             else:
                 spans = [(None, 0, CH)]
@@ -278,10 +293,9 @@ def tile_edrncell_pa_kernel(
 
         def product_fg(u):
             n, h, s = place(u)
-            z = zf[u // 4][:, s - 1 : s + 1, :]
-            nc.gpsimd.tensor_tensor(
-                out=z, in0=z, in1=a_sb[2 * h + s // 2][:, :, n * CH : (n + 1) * CH], op=MULT
-            )
+            z = zf[u // 4][:, s, :]
+            a_part = a_sb[2 * h + s // 2][:, s % 2, n * CH : (n + 1) * CH]
+            nc.gpsimd.tensor_tensor(out=z, in0=z, in1=a_part, op=MULT)
 
         def plain_gate(u, g):
             n, h, s = place(u)
@@ -361,22 +375,22 @@ def tile_edrncell_pa_kernel(
 
         v_copy, s_copy = nc.vector.tensor_copy, nc.scalar.copy
         transpose_x(0, v_copy)
+        regroup(0, 0)
         plain_fg(0)
-        plain_gate(0, 1)
         plain_fg(1)
-        plain_gate(1, 1)
+        m0 = m_to_k(0, s_copy)
+        quantise_A(0, 0)
         transpose_bias()
         plain_fg(2)
-        regroup(0, 0)
-        m0 = rows_to_k(*of_m(0), s_copy)
-        quantise_A(0, 0)
-        plain_gate(2, 1)
-        transpose_x(1, s_copy)
-        regroup(1, 0)
+        plain_gate(0, 1)
         quantise_rows(0, m0, m_codes, m_scales)
-        m1 = rows_to_k(*of_m(1), v_copy)
-        quantise_A(1, 0)
+        plain_gate(1, 1)
+        regroup(1, 0)
         plain_fg(3)
+        plain_gate(2, 1)
+        m1 = m_to_k(1, v_copy)
+        quantise_A(1, 0)
+        transpose_x(1, s_copy)
         plain_gate(3, 1)
         quantise_rows(1, m1, m_codes, m_scales)
         mask_A_th(0)
@@ -393,13 +407,13 @@ def tile_edrncell_pa_kernel(
                 mx_fg(t)
             if 0 <= t - 1 < UNITS_ALL:
                 sigmoid_fg(t - 1)
+                product_fg(t - 1)
+            if 0 <= t - 1 < UNITS_ALL:
                 activate_gate(t - 1, 1)
-                if (t - 1) % 2:
-                    product_fg(t - 1)
             if AHEAD <= t + 2 < UNITS_ALL:
                 plain_fg(t + 2)
-            if t < UNITS_ALL:
-                mx_gate(t, 1)
+            if 0 <= t - 0 < UNITS_ALL:
+                mx_gate(t - 0, 1)
             if 0 <= t - TANH_LAG < UNITS_ALL:
                 activate_gate(t - TANH_LAG, 2)
                 product_th(t - TANH_LAG)
@@ -408,7 +422,7 @@ def tile_edrncell_pa_kernel(
             back = turn_back(t - BACK) if 0 <= t - BACK else None
             if t % 2 == 1 and t // 4 < UNITS_ALL // 4:
                 transpose_a(t // 4, t % 4 // 2)
-            fresh = [(kind, j, rows_to_k(*(of_m(j) if kind == "m" else of_last(j)), v_copy)) for kind, j in row_tasks.get(t, ())]
+            fresh = [(kind, j, (m_to_k if kind == "m" else last_to_k)(j, v_copy)) for kind, j in row_tasks.get(t, ())]
             if 0 <= t - PLAIN_TH < UNITS_ALL:
                 plain_gate(t - PLAIN_TH, 2)
             for kind, j, g4 in pending:
@@ -426,16 +440,16 @@ def tile_edrncell_pa_kernel(
                 quantise_A(2, 0)
                 load_chunk(2)
             if n < NCH:
-                if s8 == 1:
+                first = 3 if n == 1 else 1
+                if s8 == (4 if n == 1 else 0):
                     mask_A_th(n)
-                if s8 == 2:
+                if s8 == (5 if n == 1 else 1):
                     regroup(2, n)
-                if 3 <= s8 < 7:
-                    regroup(0, n, s8 - 3)
-                    regroup(1, n, s8 - 3)
+                if first <= s8 < first + 4:
+                    for quarter in (2, 3) if (s8 - first) % 2 else (0, 1):
+                        regroup((s8 - first) // 2, n, quarter)
+                for g in QUANT[n == 1].get(s8, ()):
+                    quantise_A(g, n)
                 if s8 == 7:
-                    quantise_A(0, n)
-                    quantise_A(1, n)
-                    quantise_A(2, n)
                     if n + 2 < NCH:
                         load_chunk(n + 2)

@@ -50,8 +50,8 @@ def tile_edrncell_pa_kernel(
         fpool = ctx.enter_context(tc.tile_pool(name="fpool", bufs=4))
         tpool = ctx.enter_context(tc.tile_pool(name="tpool", bufs=5))
         psum_y = ctx.enter_context(tc.psum_pool(name="psum_y", bufs=3))
-        psum_x = ctx.enter_context(tc.psum_pool(name="psum_x", bufs=2))
-        psum_t = ctx.enter_context(tc.psum_pool(name="psum_t", bufs=2))
+        psum_x = ctx.enter_context(tc.psum_pool(name="psum_x", bufs=3))
+        psum_t = ctx.enter_context(tc.psum_pool(name="psum_t", bufs=1))
         psum_o = ctx.enter_context(tc.psum_pool(name="psum_o", bufs=1))
 
         x_v = x_t.rearrange("(p q) k -> p q k", q=Q)
@@ -126,8 +126,8 @@ def tile_edrncell_pa_kernel(
         load_A(1, 0)
         load_m(1)
         load_a(0)
-        load_A(2, 0)
         load_a(1)
+        load_A(2, 0)
         load_B(2, 0)
         for j in range(2, PAIRS):
             load_m(j)
@@ -345,7 +345,10 @@ def tile_edrncell_pa_kernel(
             nc.gpsimd.tensor_tensor(out=z, in0=z, in1=gate_tile(u, 1), op=MULT)
 
         def turn_back(u):
-            back = psum_o.tile([P, QH, P], F32, name="back", tag="back")
+            if u >= UNITS_ALL - CB and u % 2:
+                back = psum_t.tile([P, QH, P], F32, name="back", tag="tp")
+            else:
+                back = psum_o.tile([P, QH, P], F32, name="back", tag="back")
             for r in range(QH):
                 nc.tensor.transpose(back[:, r, :], gate_tile(u, 2)[:, r * P : (r + 1) * P], ident_f[:])
             return back
@@ -395,12 +398,7 @@ def tile_edrncell_pa_kernel(
         quantise_rows(1, m1, m_codes, m_scales)
         mask_A_th(0)
 
-        row_tasks = {
-            1: [("l", 0), ("m", 2)],
-            2: [("l", 1), ("m", 3)],
-            4: [("l", 2)],
-            5: [("l", 3)],
-        }
+        row_tasks = {1: [("l", 0)], 2: [("l", 1), ("m", 2), ("m", 3)], 4: [("l", 2)], 5: [("l", 3)]}
         pending = []
         for t in range(UNITS_ALL + BACK):
             if t < UNITS_ALL:

@@ -28,7 +28,7 @@ NCH = MD // CH
 CB = CH // P
 PAIRS = Q // 2
 UNITS_ALL = NCH * HALVES * CB
-ZBUFS = {1: 8, 2: 6}
+ZBUFS = {1: 9, 2: 6}
 QUANT = {True: {6: (0,), 7: (2, 1)}, False: {3: (0,), 5: (2,), 6: (1,)}}
 AHEAD = 4
 PLAIN_TH, MX_TH, TANH_LAG, BACK = 2, 3, 4, 7
@@ -201,7 +201,7 @@ def tile_edrncell_pa_kernel(
             return rows_to_k(*of_last(j), engine_copy)
 
         def rows_to_k(raw_tile, view, engine_copy):
-            tp = psum_t.tile([P, 2, 4, P], BF16, tag="tp")
+            tp = psum_o.tile([P, 2, 4, P], BF16, name="back", tag="back")
             for qq in range(2):
                 for t in range(4):
                     nc.tensor.transpose(tp[:, qq, t, :], view(raw_tile, qq, t), ident[:])
@@ -398,7 +398,7 @@ def tile_edrncell_pa_kernel(
         quantise_rows(1, m1, m_codes, m_scales)
         mask_A_th(0)
 
-        row_tasks = {1: [("l", 0)], 2: [("l", 1), ("m", 2), ("m", 3)], 4: [("l", 2)], 5: [("l", 3)]}
+        row_tasks = {1: [("l", 0)], 2: [("m", 2), ("l", 1), ("m", 3)], 4: [("l", 2)], 5: [("l", 3)]}
         pending = []
         for t in range(UNITS_ALL + BACK):
             if t < UNITS_ALL:
@@ -406,17 +406,17 @@ def tile_edrncell_pa_kernel(
             if 0 <= t - 1 < UNITS_ALL:
                 sigmoid_fg(t - 1)
                 product_fg(t - 1)
+            if 0 <= t - 2 < UNITS_ALL:
+                activate_gate(t - 2, 1)
+            if AHEAD <= t + 3 < UNITS_ALL:
+                plain_fg(t + 3)
             if 0 <= t - 1 < UNITS_ALL:
-                activate_gate(t - 1, 1)
-            if AHEAD <= t + 2 < UNITS_ALL:
-                plain_fg(t + 2)
-            if 0 <= t - 0 < UNITS_ALL:
-                mx_gate(t - 0, 1)
+                mx_gate(t - 1, 1)
             if 0 <= t - TANH_LAG < UNITS_ALL:
                 activate_gate(t - TANH_LAG, 2)
                 product_th(t - TANH_LAG)
-            if AHEAD <= t + 2 < UNITS_ALL:
-                plain_gate(t + 2, 1)
+            if AHEAD <= t + 3 < UNITS_ALL:
+                plain_gate(t + 3, 1)
             back = turn_back(t - BACK) if 0 <= t - BACK else None
             if t % 2 == 1 and t // 4 < UNITS_ALL // 4:
                 transpose_a(t // 4, t % 4 // 2)

@@ -117,10 +117,11 @@ def tile_edrncell_pa_kernel(
         nc.vector.memset(b_rows[:], 0.0)
         for g, b in enumerate((b_in, b_th)):
             nc.scalar.dma_start(out=b_rows[16 * g : 16 * g + 16, :], in_=b.rearrange("o (c p) -> (o c) p", p=P))
-        nc.sync.dma_start(out=x_raw[:], in_=x_v)
-        load_A(0, 0)
+        nc.sync.dma_start(out=x_raw[:, 0:QH, :], in_=x_v[:, 0:QH, :])
         load_B(0, 0)
+        load_A(0, 0)
         load_m(0)
+        nc.sync.dma_start(out=x_raw[:, QH:Q, :], in_=x_v[:, QH:Q, :])
         load_bias(0)
         load_B(1, 0)
         load_A(1, 0)
@@ -313,7 +314,7 @@ def tile_edrncell_pa_kernel(
                     start=False,
                     stop=True,
                 )
-            (nc.vector.tensor_copy if g == 1 and s == 3 else nc.scalar.copy)(out=gate_tile(u, g), in_=y[:])
+            (nc.vector.tensor_copy if g == 1 and s == 3 and u // 4 % 2 else nc.scalar.copy)(out=gate_tile(u, g), in_=y[:])
 
         def gate_tile(u, g):
             return zg[g][u][:]
@@ -404,14 +405,14 @@ def tile_edrncell_pa_kernel(
             if t < UNITS_ALL:
                 mx_fg(t)
             if 0 <= t - 1 < UNITS_ALL:
+                mx_gate(t - 1, 1)
+            if 0 <= t - 1 < UNITS_ALL:
                 sigmoid_fg(t - 1)
                 product_fg(t - 1)
             if 0 <= t - 2 < UNITS_ALL:
                 activate_gate(t - 2, 1)
             if AHEAD <= t + 3 < UNITS_ALL:
                 plain_fg(t + 3)
-            if 0 <= t - 1 < UNITS_ALL:
-                mx_gate(t - 1, 1)
             if 0 <= t - TANH_LAG < UNITS_ALL:
                 activate_gate(t - TANH_LAG, 2)
                 product_th(t - TANH_LAG)

from contextlib import ExitStack

import concourse.mybir as mybir
from concourse.masks import make_identity

F32 = mybir.dt.float32
BF16 = mybir.dt.bfloat16
U32 = mybir.dt.uint32
U8 = mybir.dt.uint8
FP8X4 = mybir.dt.float8_e4m3fn_x4
ADD = mybir.AluOpType.add
MULT = mybir.AluOpType.mult
SIGMOID = mybir.ActivationFunctionType.Sigmoid
TANH = mybir.ActivationFunctionType.Tanh
AXIS_X = mybir.AxisListType.X

P = 128
ROWS = 1024
Q = ROWS // P
HALVES = 2
QH = Q // HALVES
UNITS = 512
SLOTS = 4
MD = UNITS * SLOTS
NX = 256
CH = 512
NCH = MD // CH
CB = CH // P
PAIRS = Q // 2
UNITS_ALL = NCH * HALVES * CB
ZBUFS = {1: 9, 2: 6}
QUANT = {True: {6: (0,), 7: (2, 1)}, False: {3: (0,), 5: (2,), 6: (1,)}}
AHEAD = 4
PLAIN_TH, MX_TH, TANH_LAG, BACK = 2, 3, 4, 7

FLOPS = 2 * ROWS * MD * 3 * (UNITS + NX) + 2 * ROWS * UNITS * 6


def tile_edrncell_pa_kernel(
    tc, x_t, m_t, a_t, A_fg, A_in, A_th, A_pt_blk, B_fg, B_in, B_th, b_fg, b_in, b_th, out
):
    nc = tc.nc
    with ExitStack() as ctx:
        ctx.enter_context(tc.manual_schedule())
        const = ctx.enter_context(tc.tile_pool(name="const", bufs=1))
        raw = ctx.enter_context(tc.tile_pool(name="raw", bufs=6))
        grp = ctx.enter_context(tc.tile_pool(name="grp", bufs=4))
        wgrp = ctx.enter_context(tc.tile_pool(name="wgrp", bufs=1))
        atp = ctx.enter_context(tc.tile_pool(name="atp", bufs=2))
        fpool = ctx.enter_context(tc.tile_pool(name="fpool", bufs=4))
        tpool = ctx.enter_context(tc.tile_pool(name="tpool", bufs=5))
        psum_y = ctx.enter_context(tc.psum_pool(name="psum_y", bufs=3))
        psum_x = ctx.enter_context(tc.psum_pool(name="psum_x", bufs=3))
        psum_t = ctx.enter_context(tc.psum_pool(name="psum_t", bufs=1))
        psum_o = ctx.enter_context(tc.psum_pool(name="psum_o", bufs=1))

        x_v = x_t.rearrange("(p q) k -> p q k", q=Q)
        m_v = m_t.rearrange("(p q) k -> p q k", q=Q)
        a_v = a_t.rearrange("(p q) c -> p q c", q=Q)
        out_v = out.rearrange("(p q) c -> p q c", q=Q)
        A_v = [w.rearrange("(p t) c -> p t c", p=P) for w in (A_fg, A_in)]
        A_v.append(A_th.rearrange("(t p) c -> p t c", p=P))
        B_v = [w.rearrange("(k p) c -> p k c", p=P) for w in (B_fg, B_in, B_th)]

        ident = const.tile([P, P], BF16)
        ident_f = const.tile([P, P], F32)
        x_raw = const.tile([P, Q, NX], BF16)
        m_raw = [const.tile([P, 2, UNITS], BF16, name="m_raw%d" % j) for j in range(PAIRS)]
        a_sb = [const.tile([P, 2, MD], BF16, name="a_sb%d" % j) for j in range(PAIRS)]
        xT = [const.tile([P, 2, QH, P], BF16, name="xT%d" % h) for h in range(HALVES)]
        m_codes = [const.tile([P, QH * P], U32, name="m_codes%d" % h, align_bytes=64) for h in range(HALVES)]
        m_scales = [const.tile([P, QH * P], U8, name="m_scales%d" % h, align_bytes=64) for h in range(HALVES)]
        l_codes = [const.tile([P, QH * P], U32, name="l_codes%d" % h, align_bytes=64) for h in range(HALVES)]
        l_scales = [const.tile([P, QH * P], U8, name="l_scales%d" % h, align_bytes=64) for h in range(HALVES)]
        B_sb = [[const.tile([P, 2, CH], BF16, name="B_sb%d_%d" % (g, n)) for n in range(NCH)] for g in range(3)]
        A_codes = [
            [const.tile([P, CH], U32, name="A_codes%d_%d" % (g, n), align_bytes=64) for n in range(NCH)] for g in range(3)
        ]
        A_scales = [
            [const.tile([P, CH], U8, name="A_scales%d_%d" % (g, n), align_bytes=64) for n in range(NCH)] for g in range(3)
        ]
        bb = [const.tile([P, CH], BF16, name="bb%d" % n) for n in range(NCH)]
        b_rows = const.tile([P, P], BF16)
        b_cols = const.tile([P, 2, NCH, CB], F32)
        pt_raw = const.tile([P, 16, SLOTS], BF16)
        pt_msk = const.tile([P, 16, SLOTS], F32)
        p_blk = const.tile([P, 16, P], BF16)
        onehot = const.tile([P, SLOTS], F32)
        tri = const.tile([P, SLOTS], F32)
        same_unit = const.tile([P, P // SLOTS], F32)
        off_diag = const.tile([P, CH], BF16)

        A_raw = {}

        def load_B(g, n):
            nc.sync.dma_start(out=B_sb[g][n][:], in_=B_v[g][:, :, n * CH : (n + 1) * CH])

        def load_bias(n):
            nc.sync.dma_start(
                out=bb[n][:], in_=b_fg.rearrange("o n -> (o n)")[n * CH : (n + 1) * CH].partition_broadcast(P)
            )

        def load_A(g, n):
            a_raw = raw.tile([P, 4, CH], BF16, tag="a_raw")
            nc.sync.dma_start(out=a_raw[:], in_=A_v[g][:, :, n * CH : (n + 1) * CH])
            A_raw[(g, n)] = a_raw

        def load_m(j):
            nc.sync.dma_start(out=m_raw[j][:], in_=m_v[:, 2 * j : 2 * j + 2, :])

        def load_a(j):
            nc.sync.dma_start(out=a_sb[j][:], in_=a_v[:, 2 * j : 2 * j + 2, :])

        make_identity(nc, ident[:])
        make_identity(nc, ident_f[:])
        nc.scalar.dma_start(out=pt_raw[:], in_=A_pt_blk.rearrange("(c j) s t -> (j s) c t", j=P // SLOTS))
        nc.vector.memset(b_rows[:], 0.0)
        for g, b in enumerate((b_in, b_th)):
            nc.scalar.dma_start(out=b_rows[16 * g : 16 * g + 16, :], in_=b.rearrange("o (c p) -> (o c) p", p=P))
        nc.sync.dma_start(out=x_raw[:, 0:QH, :], in_=x_v[:, 0:QH, :])
        load_B(0, 0)
        load_A(0, 0)
        load_m(0)
        nc.sync.dma_start(out=x_raw[:, QH:Q, :], in_=x_v[:, QH:Q, :])
        load_bias(0)
        load_B(1, 0)
        load_A(1, 0)
        load_m(1)
        load_a(0)
        load_a(1)
        load_A(2, 0)
        load_B(2, 0)
        for j in range(2, PAIRS):
            load_m(j)
        for j in range(2, PAIRS):
            load_a(j)
        for g in range(3):
            load_A(g, 1)
        for g in range(3):
            load_B(g, 1)
        load_bias(1)

        nc.vector.tensor_reduce(
            out=onehot[:], in_=ident[:].rearrange("p (j s) -> p s j", s=SLOTS), axis=AXIS_X, op=ADD
        )
        nc.vector.tensor_reduce(
            out=same_unit[:], in_=ident[:].rearrange("p (j s) -> p j s", s=SLOTS), axis=AXIS_X, op=ADD
        )
        nc.vector.memset(tri[:], 0.0)
        nc.vector.tensor_copy(out=tri[:, 1:2], in_=onehot[:, 0:1])
        nc.vector.tensor_tensor(out=tri[:, 2:3], in0=tri[:, 1:2], in1=onehot[:, 1:2], op=ADD)
        nc.vector.tensor_tensor(out=tri[:, 3:4], in0=tri[:, 2:3], in1=onehot[:, 2:3], op=ADD)
        nc.gpsimd.tensor_scalar(
            out=off_diag[:].rearrange("p (i s) -> p i s", s=SLOTS),
            in0=ident[:].unsqueeze(2).to_broadcast([P, P, SLOTS]),
            scalar1=-1.0,
            scalar2=1.0,
            op0=MULT,
            op1=ADD,
        )
        nc.vector.tensor_tensor(
            out=pt_msk[:], in0=pt_raw[:], in1=tri[:].unsqueeze(1).to_broadcast([P, 16, SLOTS]), op=MULT
        )
        block = [P, 4, P // SLOTS, SLOTS]
        for n in range(NCH):
            part = slice(4 * n, 4 * n + 4)
            nc.gpsimd.tensor_tensor(
                out=p_blk[:, part, :].rearrange("p c (j t) -> p c j t", t=SLOTS),
                in0=pt_msk[:, part, :].unsqueeze(2).to_broadcast(block),
                in1=same_unit[:].unsqueeze(1).unsqueeze(3).to_broadcast(block),
                op=MULT,
            )

        def transpose_x(h, engine_copy):
            tp = psum_t.tile([P, 2, QH, P], BF16, tag="tp")
            for k in range(2):
                for r in range(QH):
                    nc.tensor.transpose(tp[:, k, r, :], x_raw[:, QH * h + r, k * P : (k + 1) * P], ident[:])
            engine_copy(out=xT[h][:], in_=tp[:])

        def transpose_bias():
            tp = psum_t.tile([P, P], BF16, tag="tp")
            nc.tensor.transpose(tp[:], b_rows[:], ident[:])
            nc.vector.tensor_copy(
                out=b_cols[:].rearrange("p g n c -> p (g n c)"), in_=tp[:, 0 : 2 * NCH * CB]
            )

        def m_to_k(j, engine_copy):
            words = m_raw[j][:].bitcast(F32)
            tp = psum_t.tile([P, 2, 2, P], F32, tag="tp")
            for qq in range(2):
                for w in range(2):
                    nc.tensor.transpose(tp[:, qq, w, :], words[:, qq, w : UNITS // 2 : 2], ident_f[:])
            g4 = grp.tile([P, 2, P, 4], BF16, tag="g4", align_bytes=64)
            engine_copy(
                out=g4[:].rearrange("p q b t -> p (q b t)").bitcast(F32).rearrange("p (q b w) -> p q b w", q=2, w=2),
                in_=tp[:].rearrange("p q w b -> p q b w"),
            )
            return g4

        def last_to_k(j, engine_copy):
            return rows_to_k(*of_last(j), engine_copy)

        def rows_to_k(raw_tile, view, engine_copy):
            tp = psum_o.tile([P, 2, 4, P], BF16, name="back", tag="back")
            for qq in range(2):
                for t in range(4):
                    nc.tensor.transpose(tp[:, qq, t, :], view(raw_tile, qq, t), ident[:])
            g4 = grp.tile([P, 2, P, 4], BF16, tag="g4", align_bytes=64)
            engine_copy(out=g4[:], in_=tp[:].rearrange("p q t b -> p q b t"))
            return g4

        def of_last(j):
            return a_sb[j], lambda tile, qq, t: tile[:, qq, :].rearrange("p (t i s) -> p t i s", t=4, s=SLOTS)[:, t, :, 3]

        def quantise_rows(j, g4, codes, scales):
            h, cols = j // 2, slice(j % 2 * 2 * P, (j % 2 + 1) * 2 * P)
            nc.vector.quantize_mx(
                out=codes[h][:, cols].bitcast(FP8X4),
                scales=scales[h][:, cols],
                in_=g4[:].rearrange("p q b t -> p (q b t)"),
            )

        grouped = {}

        def mask_A_th(n):
            a_raw = A_raw[(2, n)]
            nc.gpsimd.tensor_tensor(out=a_raw[:, n, :], in0=a_raw[:, n, :], in1=off_diag[:], op=MULT)

        def regroup(g, n, quarter=None):
            if (g, n) not in grouped:
                grouped[(g, n)] = wgrp.tile([P, CH, 4], BF16, name="grouped", tag="grouped%d" % g, align_bytes=64)
            if quarter is not None:
                spans = [(nc.scalar.copy, quarter * P, (quarter + 1) * P)]
            elif n == 0 and g < 2:
                spans = [(nc.vector.tensor_copy, 0, CH // 2), (nc.scalar.copy, CH // 2, CH)]
            else:
                spans = [(None, 0, CH)]
            for engine_copy, lo, hi in spans:
                dst = grouped[(g, n)][:, lo:hi, :].rearrange("p (c i) t -> p c t i", i=4)
                src = A_raw[(g, n)][:, :, lo:hi].rearrange("p t (c i) -> p c t i", i=4)
                if engine_copy is None:
                    nc.gpsimd.tensor_scalar(out=dst, in0=src, scalar1=1.0, scalar2=0.0, op0=MULT, op1=ADD)
                else:
                    engine_copy(out=dst, in_=src)

        def quantise_A(g, n):
            nc.vector.quantize_mx(
                out=A_codes[g][n][:].bitcast(FP8X4),
                scales=A_scales[g][n][:],
                in_=grouped[(g, n)][:].rearrange("p w t -> p (w t)"),
            )

        def load_chunk(n):
            for g in range(3):
                load_A(g, n)
            for g in range(3):
                load_B(g, n)
            load_bias(n)

        zf, zg, aT = {}, {1: {}, 2: {}}, {}

        def place(u):
            return u // 8, u // 4 % 2, u % 4

        def plain_fg(u):
            n, h, s = place(u)
            if s == 0:
                zf[u // 4] = fpool.tile([P, QH, CH], F32, name="zf", tag="zf")
            y = psum_y.tile([P, CH], F32, tag="y")
            for k in range(2):
                nc.tensor.matmul(y[:], lhsT=xT[h][:, k, s, :], rhs=B_sb[0][n][:, k, :], start=(k == 0), stop=(k == 1))
            nc.vector.tensor_tensor(out=zf[u // 4][:, s, :], in0=y[:], in1=bb[n][:], op=ADD)

        def mx_fg(u):
            n, h, s = place(u)
            rows = slice(s * P, (s + 1) * P)
            acc = psum_x.tile([P, CH], F32, tag="acc")
            nc.tensor.matmul_mx(
                out=acc[:],
                lhsT=m_codes[h][:, rows].bitcast(FP8X4),
                lhsT_scale=m_scales[h][:, rows],
                rhs=A_codes[0][n][:].bitcast(FP8X4),
                rhs_scale=A_scales[0][n][:],
                start=True,
                stop=True,
            )
            z = zf[u // 4][:, s, :]
            nc.vector.tensor_tensor(out=z, in0=acc[:], in1=z, op=ADD)

        def sigmoid_fg(u):
            z = zf[u // 4][:, u % 4, :]
            nc.scalar.activation(out=z, in_=z, func=SIGMOID)

        def product_fg(u):
            n, h, s = place(u)
            z = zf[u // 4][:, s, :]
            a_part = a_sb[2 * h + s // 2][:, s % 2, n * CH : (n + 1) * CH]
            nc.gpsimd.tensor_tensor(out=z, in0=z, in1=a_part, op=MULT)

        def plain_gate(u, g):
            n, h, s = place(u)
            cols = slice(s * P, (s + 1) * P)
            zg[g][u] = tpool.tile([P, QH * P], F32, name="zg%d" % g, tag="zg%d" % g, bufs=ZBUFS[g])
            y = psum_y.tile([P, QH * P], F32, tag="y")
            x_k = [xT[h][:, k, :, :].rearrange("p r b -> p (r b)") for k in range(2)]
            nc.tensor.matmul(y[:], lhsT=B_sb[g][n][:, 0, cols], rhs=x_k[0], start=True, stop=False)
            nc.tensor.matmul(y[:], lhsT=B_sb[g][n][:, 1, cols], rhs=x_k[1], start=False, stop=(g == 1))
            if g == 2:
                nc.tensor.matmul(
                    y[:],
                    lhsT=p_blk[:, CB * n + s, :],
                    rhs=aT[u // 4][:, s, :, :].rearrange("p r b -> p (r b)"),
                    start=False,
                    stop=True,
                )
            (nc.vector.tensor_copy if g == 1 and s == 3 and u // 4 % 2 else nc.scalar.copy)(out=gate_tile(u, g), in_=y[:])

        def gate_tile(u, g):
            return zg[g][u][:]

        def mx_gate(u, g):
            n, h, s = place(u)
            cols = slice(s * P, (s + 1) * P)
            acc = psum_x.tile([P, QH * P], F32, tag="acc")
            codes, scales = (m_codes, m_scales) if g == 1 else (l_codes, l_scales)
            nc.tensor.matmul_mx(
                out=acc[:],
                lhsT=A_codes[g][n][:, cols].bitcast(FP8X4),
                lhsT_scale=A_scales[g][n][:, cols],
                rhs=codes[h][:].bitcast(FP8X4),
                rhs_scale=scales[h][:],
                start=True,
                stop=True,
            )
            z = gate_tile(u, g)
            nc.vector.tensor_tensor(out=z, in0=acc[:], in1=z, op=ADD)

        def activate_gate(u, g):
            n, h, s = place(u)
            z = gate_tile(u, g)
            nc.scalar.activation(out=z, in_=z, func=SIGMOID if g == 1 else TANH, bias=b_cols[:, g - 1, n, s : s + 1])

        def product_th(u):
            z = gate_tile(u, 2)
            nc.gpsimd.tensor_tensor(out=z, in0=z, in1=gate_tile(u, 1), op=MULT)

        def turn_back(u):
            if u >= UNITS_ALL - CB and u % 2:
                back = psum_t.tile([P, QH, P], F32, name="back", tag="tp")
            else:
                back = psum_o.tile([P, QH, P], F32, name="back", tag="back")
            for r in range(QH):
                nc.tensor.transpose(back[:, r, :], gate_tile(u, 2)[:, r * P : (r + 1) * P], ident_f[:])
            return back

        def total(u, back):
            n, h, s = place(u)
            z = zf[u // 4][:, :, s * P : (s + 1) * P]
            nc.vector.tensor_tensor(out=z, in0=back[:], in1=z, op=ADD)
            width = P if u // 4 == UNITS_ALL // 4 - 1 else 2 * P
            if (s + 1) * P % width == 0:
                lo = (s + 1) * P - width
                nc.sync.dma_start(
                    out=out_v[:, QH * h : QH * (h + 1), n * CH + lo : n * CH + lo + width],
                    in_=zf[u // 4][:, :, lo : lo + width],
                )

        def transpose_a(macro, part):
            n, h = macro // 2, macro % 2
            if part == 0:
                aT[macro] = atp.tile([P, CB, QH, P], BF16, name="aT", tag="aT")
            tp = psum_t.tile([P, 2, QH, P], BF16, tag="tp")
            for c in range(2):
                col = n * CH + (2 * part + c) * P
                for r in range(QH):
                    nc.tensor.transpose(tp[:, c, r, :], a_sb[2 * h + r // 2][:, r % 2, col : col + P], ident[:])
            nc.scalar.copy(out=aT[macro][:, 2 * part : 2 * part + 2, :, :], in_=tp[:])

        v_copy, s_copy = nc.vector.tensor_copy, nc.scalar.copy
        transpose_x(0, v_copy)
        regroup(0, 0)
        plain_fg(0)
        plain_fg(1)
        m0 = m_to_k(0, s_copy)
        quantise_A(0, 0)
        transpose_bias()
        plain_fg(2)
        plain_gate(0, 1)
        quantise_rows(0, m0, m_codes, m_scales)
        plain_gate(1, 1)
        regroup(1, 0)
        plain_fg(3)
        plain_gate(2, 1)
        m1 = m_to_k(1, v_copy)
        quantise_A(1, 0)
        transpose_x(1, s_copy)
        plain_gate(3, 1)
        quantise_rows(1, m1, m_codes, m_scales)
        mask_A_th(0)

        row_tasks = {1: [("l", 0)], 2: [("m", 2), ("l", 1), ("m", 3)], 4: [("l", 2)], 5: [("l", 3)]}
        pending = []
        for t in range(UNITS_ALL + BACK):
            if t < UNITS_ALL:
                mx_fg(t)
            if 0 <= t - 1 < UNITS_ALL:
                mx_gate(t - 1, 1)
            if 0 <= t - 1 < UNITS_ALL:
                sigmoid_fg(t - 1)
                product_fg(t - 1)
            if 0 <= t - 2 < UNITS_ALL:
                activate_gate(t - 2, 1)
            if AHEAD <= t + 3 < UNITS_ALL:
                plain_fg(t + 3)
            if 0 <= t - TANH_LAG < UNITS_ALL:
                activate_gate(t - TANH_LAG, 2)
                product_th(t - TANH_LAG)
            if AHEAD <= t + 3 < UNITS_ALL:
                plain_gate(t + 3, 1)
            back = turn_back(t - BACK) if 0 <= t - BACK else None
            if t % 2 == 1 and t // 4 < UNITS_ALL // 4:
                transpose_a(t // 4, t % 4 // 2)
            fresh = [(kind, j, (m_to_k if kind == "m" else last_to_k)(j, v_copy)) for kind, j in row_tasks.get(t, ())]
            if 0 <= t - PLAIN_TH < UNITS_ALL:
                plain_gate(t - PLAIN_TH, 2)
            for kind, j, g4 in pending:
                codes, scales = (m_codes, m_scales) if kind == "m" else (l_codes, l_scales)
                quantise_rows(j, g4, codes, scales)
            pending = fresh
            if back is not None:
                total(t - BACK, back)
            if 0 <= t - MX_TH < UNITS_ALL:
                mx_gate(t - MX_TH, 2)
            n, s8 = t // 8 + 1, t % 8
            if t == 1:
                regroup(2, 0)
            if t == 2:
                quantise_A(2, 0)
                load_chunk(2)
            if n < NCH:
                first = 3 if n == 1 else 1
                if s8 == (4 if n == 1 else 0):
                    mask_A_th(n)
                if s8 == (5 if n == 1 else 1):
                    regroup(2, n)
                if first <= s8 < first + 4:
                    for quarter in (2, 3) if (s8 - first) % 2 else (0, 1):
                        regroup((s8 - first) // 2, n, quarter)
                for g in QUANT[n == 1].get(s8, ()):
                    quantise_A(g, n)
                if s8 == 7:
                    if n + 2 < NCH:
                        load_chunk(n + 2)
